import numpy as np
import ml_dtypes


def mxq(x, axis, fmt="e4m3"):
    dtype, down = {"e4m3": (ml_dtypes.float8_e4m3fn, 7), "e5m2": (ml_dtypes.float8_e5m2, 14)}[fmt]
    v = np.moveaxis(np.asarray(x, np.float32).astype(ml_dtypes.bfloat16).astype(np.float64), axis, -1)
    blocks = v.reshape(v.shape[:-1] + (-1, 32))
    amax = np.abs(blocks).max(-1, keepdims=True)
    byte = np.maximum(np.where(amax > 0, np.frexp(amax)[1] - 1 + 127, 0) - down, 1)
    scale = np.exp2(byte - 127.0)
    codes = (blocks / scale).astype(np.float32).astype(dtype).astype(np.float64)
    return np.moveaxis((codes * scale).reshape(v.shape), -1, axis)


WIDE = False


def mx_kscale(k):
    if not WIDE:
        return np.ones(k)
    levels = np.array([10, -10, 5, -5, 0])
    a = np.random.permutation(np.resize(levels, k // 512 * 4)).reshape(k // 512, 4)
    idx = np.arange(k)
    return np.exp2(a[idx // 512, idx % 128 // 32])


BF16 = ml_dtypes.bfloat16


def bf(x):
    return np.asarray(x, np.float32).astype(BF16)


def f64(x):
    return np.asarray(x).astype(np.float64)


B, T, D, H, HD, Q_STRIDE, WINDOW, QKV = 1, 1536, 1024, 16, 64, 4, 128, 3
NW = T // (Q_STRIDE * WINDOW)
SEQ = T // NW


def setup_inputs():
    s = mx_kscale(D)
    return {"embeddings": bf(np.random.standard_normal((B, T, D)) * s),
            "qkv_w": bf(np.random.standard_normal((QKV * D, D)) / np.sqrt(D) / s[None, :]),
            "qkv_b": bf(np.random.standard_normal(QKV * D) * 0.3)}


def reference(embeddings, qkv_w, qkv_b):
    y = (mxq(f64(embeddings), 2, "e4m3") @ mxq(f64(qkv_w), 1, "e4m3").T) + f64(qkv_b)
    qkv = y.reshape(B, SEQ, NW, QKV, H, HD)
    qkv = qkv.transpose(3, 0, 4, 2, 1, 5)
    q, k, v = qkv[0], qkv[1], qkv[2]
    q = q.reshape(B, H, NW, Q_STRIDE, SEQ // Q_STRIDE, HD).max(axis=3)
    return q, k, v

@@ -1,0 +1,263 @@
+from contextlib import ExitStack
+
+import concourse.mybir as mybir
+from concourse.masks import make_identity
+
+F32 = mybir.dt.float32
+BF16 = mybir.dt.bfloat16
+U32 = mybir.dt.uint32
+U8 = mybir.dt.uint8
+FP8X4 = mybir.dt.float8_e4m3fn_x4
+ADD = mybir.AluOpType.add
+MAX = mybir.AluOpType.max
+AXIS_X = mybir.AxisListType.X
+
+P = 128
+FLOPS = 2 * 1536 * 3072 * 1024
+
+PINNED = True
+
+
+def tile_hieramaskunitattention_pa_kernel(tc, embeddings, qkv_w, qkv_b, out_0, out_1, out_2):
+    nc = tc.nc
+    x_rows = embeddings.flatten_outer_dims().rearrange("(p j w) k -> w p j k", j=4, w=3)
+
+    with ExitStack() as ctx:
+        const = ctx.enter_context(tc.tile_pool(name="const", bufs=1))
+        raw_pool = ctx.enter_context(tc.tile_pool(name="raw", bufs=6))
+        grp_pool = ctx.enter_context(tc.tile_pool(name="grp", bufs=3))
+        code_pool = ctx.enter_context(tc.tile_pool(name="code", bufs=1))
+        out_pool = ctx.enter_context(tc.tile_pool(name="outp", bufs=9))
+        qo_pool = ctx.enter_context(tc.tile_pool(name="qo", bufs=3))
+        tp_pool = ctx.enter_context(tc.psum_pool(name="tp", bufs=4))
+        acc_pool = ctx.enter_context(tc.psum_pool(name="acc", bufs=4))
+        if PINNED:
+            ctx.enter_context(tc.manual_schedule())
+
+        raws = {}
+        grouped = {}
+        codes = {}
+        planes = {}
+
+        def source(key):
+            kind, idx = key
+            if kind == "x":
+                return x_rows[idx]
+            return qkv_w[512 * idx : 512 * idx + 512, :].rearrange("(t p) k -> p t k", p=P)
+
+        def load(key, pieces):
+            raw = raw_pool.tile([P, 4096], BF16, name="raw")
+            raws[key] = raw
+            view = raw[:].rearrange("p (t k) -> p t k", t=4)
+            src = source(key)
+            step = 4 // pieces
+            for a in range(0, 4, step):
+                nc.sync.dma_start(out=view[:, a : a + step, :], in_=src[:, a : a + step, :])
+
+        def begin_group(key):
+            grouped[key] = grp_pool.tile([P, 4096], BF16, name="grouped", align_bytes=64)
+            codes[key] = code_pool.tile([P, 1024], U32, name="codes_%s%d" % key, align_bytes=64)
+            planes[key] = code_pool.tile([P, 1024], U8, name="plane_%s%d" % key, align_bytes=64)
+
+        def transpose_tile(key, t, engine):
+            words = raws[key][:].bitcast(F32)
+            bank = tp_pool.tile([P, 512], F32, name="bank")
+            for gu in range(4):
+                nc.tensor.transpose(
+                    bank[:, gu * P : (gu + 1) * P],
+                    words[:, t * 512 + gu * P : t * 512 + (gu + 1) * P],
+                    ident[:],
+                )
+            dst = grouped[key][:].bitcast(F32).rearrange("p (g t n u) -> p g t n u", g=2, t=4, n=P, u=2)
+            src = bank[:].rearrange("p (g u n) -> p g n u", g=2, u=2, n=P)
+            if engine == "S":
+                nc.scalar.copy(out=dst[:, :, t, :, :], in_=src)
+            else:
+                nc.vector.tensor_copy(out=dst[:, :, t, :, :], in_=src)
+
+        def quantise(key, first, width):
+            nc.vector.quantize_mx(
+                out=codes[key][:, first : first + width].bitcast(FP8X4),
+                scales=planes[key][:, first : first + width],
+                in_=grouped[key][:, 4 * first : 4 * (first + width)],
+            )
+
+        def quantise_tile(key, t):
+            for g in range(2):
+                quantise(key, g * 512 + t * P, P)
+
+        def prepare_fine(key, engines):
+            begin_group(key)
+            for t in range(4):
+                transpose_tile(key, t, engines[t])
+                if t > 0:
+                    quantise_tile(key, t - 1)
+            quantise_tile(key, 3)
+
+        def prepare(key, engines):
+            begin_group(key)
+            for t in range(4):
+                transpose_tile(key, t, engines[t])
+
+        def quantise_halves(key):
+            quantise(key, 0, 512)
+            quantise(key, 512, 512)
+
+        def quantise_whole(key):
+            quantise(key, 0, 1024)
+
+        def mx_pair(acc, stat_key, stat_col, mov_key):
+            for g in range(2):
+                s0 = g * 512 + stat_col
+                nc.tensor.matmul_mx(
+                    out=acc[:],
+                    lhsT=codes[stat_key][:, s0 : s0 + P].bitcast(FP8X4),
+                    lhsT_scale=planes[stat_key][:, s0 : s0 + P],
+                    rhs=codes[mov_key][:, g * 512 : (g + 1) * 512].bitcast(FP8X4),
+                    rhs_scale=planes[mov_key][:, g * 512 : (g + 1) * 512],
+                    start=(g == 0),
+                    stop=(g == 1),
+                )
+
+        def kv_unit(grp, w, engines):
+            dram = out_1 if grp < 4 else out_2
+            h0 = 8 * (grp % 2)
+            res = out_pool.tile([P, 2048], F32, name="res")
+            res_v = res[:].rearrange("p (h j d) -> p h j d", h=8, j=4, d=64)
+            bias_v = bias[:, grp * 512 : (grp + 1) * 512].rearrange("p (h d) -> p h d", h=8)
+            accs = []
+            for j in range(4):
+                acc = acc_pool.tile([P, 512], F32, name="acc")
+                mx_pair(acc, ("x", w), j * P, ("w", grp))
+                accs.append(acc)
+            for j in range(4):
+                acc_v = accs[j][:].rearrange("p (h d) -> p h d", h=8)
+                if engines[j] == "V":
+                    nc.vector.tensor_tensor(out=res_v[:, :, j, :], in0=acc_v, in1=bias_v, op=ADD)
+                else:
+                    nc.scalar.copy(out=res_v[:, :, j, :], in_=acc_v)
+                    nc.gpsimd.tensor_tensor(out=res_v[:, :, j, :], in0=res_v[:, :, j, :], in1=bias_v, op=ADD)
+            nc.sync.dma_start(
+                out=dram[0, h0 : h0 + 8, w, :, :].rearrange("h (p j) d -> p h (j d)", j=4),
+                in_=res[:].rearrange("p (h e) -> p h e", h=8),
+            )
+
+        def q_unit(c8):
+            for w in range(3):
+                acc = acc_pool.tile([P, 512], F32, name="acc")
+                mx_pair(acc, ("w", c8 // 4), (c8 % 4) * P, ("x", w))
+                nc.vector.tensor_reduce(
+                    out=pooled_v[:, 4 * c8 : 4 * c8 + 4, w, :],
+                    in_=acc[:].rearrange("p (j g q) -> p j q g", j=4, g=4, q=32),
+                    axis=AXIS_X,
+                    op=MAX,
+                )
+
+        def q_transposes(c8):
+            bank = tp_pool.tile([P, 512], F32, name="bank")
+            for j in range(4):
+                nc.tensor.transpose(
+                    bank[:, j * P : (j + 1) * P],
+                    pooled[:, c8 * 512 + j * P : c8 * 512 + (j + 1) * P],
+                    ident[:],
+                )
+            return bank
+
+        def q_finish(c8, bank, engine):
+            qo = qo_pool.tile([P, 512], F32, name="qo")
+            qo_v = qo[0:96, :].rearrange("p (h j d) -> p h j d", h=2, j=4, d=64)
+            bank_v = bank[0:96, :].rearrange("p (j h d) -> p h j d", j=4, h=2, d=64)
+            bias_v = (
+                bias[0:96, c8 * P : (c8 + 1) * P]
+                .rearrange("p (h d) -> p h d", h=2)
+                .unsqueeze(2)
+                .to_broadcast([96, 2, 4, 64])
+            )
+            if engine == "V":
+                nc.vector.tensor_tensor(out=qo_v, in0=bank_v, in1=bias_v, op=ADD)
+            else:
+                nc.scalar.copy(out=qo_v, in_=bank_v)
+                nc.gpsimd.tensor_tensor(out=qo_v, in0=qo_v, in1=bias_v, op=ADD)
+            nc.sync.dma_start(
+                out=out_0[0, 2 * c8 : 2 * c8 + 2, :, :, :].rearrange("h w (q j) d -> (w q) h (j d)", j=4),
+                in_=qo[0:96, :].rearrange("p (h e) -> p h e", h=2),
+            )
+
+        bias_rows = const.tile([P, 512], BF16, name="bias_rows")
+        ident_bf = const.tile([P, P], BF16, name="ident_bf")
+        ident = const.tile([P, P], F32, name="ident")
+        bias = const.tile([P, 3072], F32, name="bias")
+        pooled = const.tile([P, 4096], F32, name="pooled")
+        pooled_v = pooled[:].rearrange("p (a s q) -> p a s q", a=32, s=4, q=32)
+
+        nc.vector.memset(bias_rows[:], 0.0)
+        nc.scalar.dma_start(out=bias_rows[0:6, :], in_=qkv_b.rearrange("(n c) -> n c", n=6))
+        load(("w", 2), 4)
+        load(("x", 0), 4)
+        load(("x", 1), 2)
+        load(("x", 2), 1)
+        load(("w", 3), 1)
+        load(("w", 0), 1)
+        make_identity(nc, ident[:])
+        make_identity(nc, ident_bf[:])
+        nc.gpsimd.memset(pooled_v[:, :, 3, :], 0.0)
+
+        def spread_bias(n, engine):
+            acc = acc_pool.tile([P, 512], F32, name="acc")
+            nc.tensor.matmul(
+                acc[:], lhsT=ident_bf[:, n : n + 1].to_broadcast([P, P]), rhs=bias_rows[:], start=True, stop=True
+            )
+            if engine == "V":
+                nc.vector.tensor_copy(out=bias[:, n * 512 : (n + 1) * 512], in_=acc[:])
+            else:
+                nc.scalar.copy(out=bias[:, n * 512 : (n + 1) * 512], in_=acc[:])
+
+        prepare_fine(("w", 2), "SVSV")
+        spread_bias(2, "V")
+        spread_bias(3, "S")
+        load(("w", 4), 1)
+        prepare_fine(("x", 0), "SVSV")
+        load(("w", 5), 1)
+        kv_unit(2, 0, "VSVS")
+        prepare_fine(("x", 1), "SVSV")
+        load(("w", 1), 1)
+        kv_unit(2, 1, "VSVS")
+        prepare_fine(("x", 2), "SVSV")
+        prepare(("w", 3), "SVSV")
+        spread_bias(4, "V")
+        spread_bias(5, "S")
+        quantise_halves(("w", 3))
+        kv_unit(2, 2, "VSVV")
+        kv_unit(3, 0, "VSVS")
+        prepare(("w", 0), "SSSS")
+        spread_bias(0, "V")
+        spread_bias(1, "V")
+        kv_unit(3, 1, "VSVS")
+        quantise_whole(("w", 0))
+        kv_unit(3, 2, "VSVV")
+        q_unit(0)
+        q_unit(1)
+        prepare(("w", 4), "SSSS")
+        q_unit(2)
+        quantise_whole(("w", 4))
+        q_unit(3)
+        kv_unit(4, 0, "VSVS")
+        banks = [q_transposes(c8) for c8 in range(4)]
+        for c8 in range(4):
+            q_finish(c8, banks[c8], "S")
+        prepare(("w", 5), "SSSS")
+        kv_unit(4, 1, "VSVS")
+        quantise_whole(("w", 5))
+        kv_unit(4, 2, "VSVV")
+        kv_unit(5, 0, "VSVS")
+        prepare(("w", 1), "SSSS")
+        kv_unit(5, 1, "VSVS")
+        quantise_whole(("w", 1))
+        kv_unit(5, 2, "VSVV")
+        for c8 in range(4, 8):
+            q_unit(c8)
+        banks = [q_transposes(c8) for c8 in range(4, 8)]
+        q_finish(4, banks[0], "S")
+        q_finish(5, banks[1], "V")
+        q_finish(6, banks[2], "V")
+        q_finish(7, banks[3], "V")

@@ -137,10 +137,12 @@ def tile_hieramaskunitattention_pa_kernel(tc, embeddings, qkv_w, qkv_b, out_0, o
                 else:
                     nc.scalar.copy(out=res_v[:, :, j, :], in_=acc_v)
                     nc.gpsimd.tensor_tensor(out=res_v[:, :, j, :], in0=res_v[:, :, j, :], in1=bias_v, op=ADD)
-            nc.sync.dma_start(
-                out=dram[0, h0 : h0 + 8, w, :, :].rearrange("h (p j) d -> p h (j d)", j=4),
-                in_=res[:].rearrange("p (h e) -> p h e", h=8),
-            )
+            res_h = res[:].rearrange("p (h e) -> p h e", h=8)
+            for a in (0, 4):
+                nc.sync.dma_start(
+                    out=dram[0, h0 + a : h0 + a + 4, w, :, :].rearrange("h (p j) d -> p h (j d)", j=4),
+                    in_=res_h[:, a : a + 4, :],
+                )
 
         def q_unit(c8):
             for w in range(3):

@@ -27,8 +27,8 @@ def tile_hieramaskunitattention_pa_kernel(tc, embeddings, qkv_w, qkv_b, out_0, o
         raw_pool = ctx.enter_context(tc.tile_pool(name="raw", bufs=6))
         grp_pool = ctx.enter_context(tc.tile_pool(name="grp", bufs=3))
         code_pool = ctx.enter_context(tc.tile_pool(name="code", bufs=1))
-        out_pool = ctx.enter_context(tc.tile_pool(name="outp", bufs=9))
-        qo_pool = ctx.enter_context(tc.tile_pool(name="qo", bufs=3))
+        out_pool = ctx.enter_context(tc.tile_pool(name="outp", bufs=8))
+        qo_pool = ctx.enter_context(tc.tile_pool(name="qo", bufs=6))
         tp_pool = ctx.enter_context(tc.psum_pool(name="tp", bufs=4))
         acc_pool = ctx.enter_context(tc.psum_pool(name="acc", bufs=4))
         if PINNED:
@@ -38,6 +38,7 @@ def tile_hieramaskunitattention_pa_kernel(tc, embeddings, qkv_w, qkv_b, out_0, o
         grouped = {}
         codes = {}
         planes = {}
+        results = {}
 
         def source(key):
             kind, idx = key
@@ -119,30 +120,33 @@ def tile_hieramaskunitattention_pa_kernel(tc, embeddings, qkv_w, qkv_b, out_0, o
                     stop=(g == 1),
                 )
 
-        def kv_unit(grp, w, engines):
+        def kv_unit(grp, w, engines, tiles=(0, 1, 2, 3)):
             dram = out_1 if grp < 4 else out_2
             h0 = 8 * (grp % 2)
-            res = out_pool.tile([P, 2048], F32, name="res")
+            if (grp, w) not in results:
+                results[(grp, w)] = out_pool.tile([P, 2048], F32, name="res")
+            res = results[(grp, w)]
             res_v = res[:].rearrange("p (h j d) -> p h j d", h=8, j=4, d=64)
             bias_v = bias[:, grp * 512 : (grp + 1) * 512].rearrange("p (h d) -> p h d", h=8)
-            accs = []
-            for j in range(4):
+            accs = {}
+            for j in tiles:
                 acc = acc_pool.tile([P, 512], F32, name="acc")
                 mx_pair(acc, ("x", w), j * P, ("w", grp))
-                accs.append(acc)
-            for j in range(4):
+                accs[j] = acc
+            for j in tiles:
                 acc_v = accs[j][:].rearrange("p (h d) -> p h d", h=8)
                 if engines[j] == "V":
                     nc.vector.tensor_tensor(out=res_v[:, :, j, :], in0=acc_v, in1=bias_v, op=ADD)
                 else:
                     nc.scalar.copy(out=res_v[:, :, j, :], in_=acc_v)
                     nc.gpsimd.tensor_tensor(out=res_v[:, :, j, :], in0=res_v[:, :, j, :], in1=bias_v, op=ADD)
-            res_h = res[:].rearrange("p (h e) -> p h e", h=8)
-            for a in (0, 4):
-                nc.sync.dma_start(
-                    out=dram[0, h0 + a : h0 + a + 4, w, :, :].rearrange("h (p j) d -> p h (j d)", j=4),
-                    in_=res_h[:, a : a + 4, :],
-                )
+            if 3 in tiles:
+                res_h = res[:].rearrange("p (h e) -> p h e", h=8)
+                for a in (0, 4):
+                    nc.sync.dma_start(
+                        out=dram[0, h0 + a : h0 + a + 4, w, :, :].rearrange("h (p j) d -> p h (j d)", j=4),
+                        in_=res_h[:, a : a + 4, :],
+                    )
 
         def q_unit(c8):
             for w in range(3):
@@ -197,8 +201,8 @@ def tile_hieramaskunitattention_pa_kernel(tc, embeddings, qkv_w, qkv_b, out_0, o
         load(("w", 2), 4)
         load(("x", 0), 4)
         load(("x", 1), 2)
-        load(("x", 2), 1)
-        load(("w", 3), 1)
+        load(("x", 2), 2)
+        load(("w", 3), 2)
         load(("w", 0), 1)
         make_identity(nc, ident[:])
         make_identity(nc, ident_bf[:])
@@ -214,52 +218,61 @@ def tile_hieramaskunitattention_pa_kernel(tc, embeddings, qkv_w, qkv_b, out_0, o
             else:
                 nc.scalar.copy(out=bias[:, n * 512 : (n + 1) * 512], in_=acc[:])
 
-        prepare_fine(("w", 2), "SVSV")
+        def finish(units, engines):
+            banks = [q_transposes(c8) for c8 in units]
+            for i in range(len(units)):
+                q_finish(units[i], banks[i], engines[i])
+
+        EARLY = "SVSS"
+        LATE = "SSSS"
+        KV = "VSVS"
+        first, second = (0, 1), (2, 3)
+        prepare_fine(("w", 2), EARLY)
+        load(("w", 4), 1)
+        prepare_fine(("x", 0), EARLY)
+        load(("w", 5), 1)
         spread_bias(2, "V")
         spread_bias(3, "S")
-        load(("w", 4), 1)
-        prepare_fine(("x", 0), "SVSV")
-        load(("w", 5), 1)
-        kv_unit(2, 0, "VSVS")
-        prepare_fine(("x", 1), "SVSV")
+        kv_unit(2, 0, KV, first)
+        prepare_fine(("x", 1), EARLY)
         load(("w", 1), 1)
-        kv_unit(2, 1, "VSVS")
-        prepare_fine(("x", 2), "SVSV")
-        prepare(("w", 3), "SVSV")
+        kv_unit(2, 0, KV, second)
+        kv_unit(2, 1, KV, first)
+        prepare_fine(("x", 2), EARLY)
+        kv_unit(2, 1, KV, second)
+        kv_unit(2, 2, KV, first)
+        prepare_fine(("w", 3), EARLY)
         spread_bias(4, "V")
         spread_bias(5, "S")
-        quantise_halves(("w", 3))
-        kv_unit(2, 2, "VSVV")
-        kv_unit(3, 0, "VSVS")
-        prepare(("w", 0), "SSSS")
+        kv_unit(2, 2, KV, second)
+        kv_unit(3, 0, KV)
+        prepare(("w", 0), LATE)
         spread_bias(0, "V")
-        spread_bias(1, "V")
-        kv_unit(3, 1, "VSVS")
+        spread_bias(1, "S")
+        kv_unit(3, 1, KV)
         quantise_whole(("w", 0))
-        kv_unit(3, 2, "VSVV")
+        prepare(("w", 4), LATE)
+        kv_unit(3, 2, KV)
+        quantise_whole(("w", 4))
         q_unit(0)
         q_unit(1)
-        prepare(("w", 4), "SSSS")
+        kv_unit(4, 0, KV)
         q_unit(2)
-        quantise_whole(("w", 4))
-        q_unit(3)
-        kv_unit(4, 0, "VSVS")
-        banks = [q_transposes(c8) for c8 in range(4)]
-        for c8 in range(4):
-            q_finish(c8, banks[c8], "S")
-        prepare(("w", 5), "SSSS")
-        kv_unit(4, 1, "VSVS")
+        finish((0, 1), "SV")
+        prepare(("w", 5), LATE)
+        kv_unit(4, 1, KV)
         quantise_whole(("w", 5))
-        kv_unit(4, 2, "VSVV")
-        kv_unit(5, 0, "VSVS")
-        prepare(("w", 1), "SSSS")
-        kv_unit(5, 1, "VSVS")
+        q_unit(3)
+        kv_unit(4, 2, KV)
+        finish((2, 3), "SV")
+        prepare(("w", 1), LATE)
+        kv_unit(5, 0, KV)
         quantise_whole(("w", 1))
-        kv_unit(5, 2, "VSVV")
-        for c8 in range(4, 8):
-            q_unit(c8)
-        banks = [q_transposes(c8) for c8 in range(4, 8)]
-        q_finish(4, banks[0], "S")
-        q_finish(5, banks[1], "V")
-        q_finish(6, banks[2], "V")
-        q_finish(7, banks[3], "V")
+        kv_unit(5, 1, KV)
+        q_unit(4)
+        kv_unit(5, 2, KV)
+        q_unit(5)
+        q_unit(6)
+        finish((4, 5), "SV")
+        q_unit(7)
+        finish((6, 7), "VV")

@@ -29,8 +29,7 @@ def tile_hieramaskunitattention_pa_kernel(tc, embeddings, qkv_w, qkv_b, out_0, o
         code_pool = ctx.enter_context(tc.tile_pool(name="code", bufs=1))
         out_pool = ctx.enter_context(tc.tile_pool(name="outp", bufs=8))
         qo_pool = ctx.enter_context(tc.tile_pool(name="qo", bufs=6))
-        tp_pool = ctx.enter_context(tc.psum_pool(name="tp", bufs=4))
-        acc_pool = ctx.enter_context(tc.psum_pool(name="acc", bufs=4))
+        psum = ctx.enter_context(tc.psum_pool(name="psum", bufs=8))
         if PINNED:
             ctx.enter_context(tc.manual_schedule())
 
@@ -62,7 +61,7 @@ def tile_hieramaskunitattention_pa_kernel(tc, embeddings, qkv_w, qkv_b, out_0, o
 
         def transpose_tile(key, t, engine):
             words = raws[key][:].bitcast(F32)
-            bank = tp_pool.tile([P, 512], F32, name="bank")
+            bank = psum.tile([P, 512], F32, name="bank")
             for gu in range(4):
                 nc.tensor.transpose(
                     bank[:, gu * P : (gu + 1) * P],
@@ -120,7 +119,7 @@ def tile_hieramaskunitattention_pa_kernel(tc, embeddings, qkv_w, qkv_b, out_0, o
                     stop=(g == 1),
                 )
 
-        def kv_unit(grp, w, engines, tiles=(0, 1, 2, 3)):
+        def kv_unit(grp, w, engines, tiles=(0, 1, 2, 3), between=None):
             dram = out_1 if grp < 4 else out_2
             h0 = 8 * (grp % 2)
             if (grp, w) not in results:
@@ -130,7 +129,7 @@ def tile_hieramaskunitattention_pa_kernel(tc, embeddings, qkv_w, qkv_b, out_0, o
             bias_v = bias[:, grp * 512 : (grp + 1) * 512].rearrange("p (h d) -> p h d", h=8)
             accs = {}
             for j in tiles:
-                acc = acc_pool.tile([P, 512], F32, name="acc")
+                acc = psum.tile([P, 512], F32, name="bank")
                 mx_pair(acc, ("x", w), j * P, ("w", grp))
                 accs[j] = acc
             for j in tiles:
@@ -140,6 +139,8 @@ def tile_hieramaskunitattention_pa_kernel(tc, embeddings, qkv_w, qkv_b, out_0, o
                 else:
                     nc.scalar.copy(out=res_v[:, :, j, :], in_=acc_v)
                     nc.gpsimd.tensor_tensor(out=res_v[:, :, j, :], in0=res_v[:, :, j, :], in1=bias_v, op=ADD)
+                if between is not None and j == tiles[0]:
+                    quantise_whole(between)
             if 3 in tiles:
                 res_h = res[:].rearrange("p (h e) -> p h e", h=8)
                 for a in (0, 4):
@@ -150,7 +151,7 @@ def tile_hieramaskunitattention_pa_kernel(tc, embeddings, qkv_w, qkv_b, out_0, o
 
         def q_unit(c8):
             for w in range(3):
-                acc = acc_pool.tile([P, 512], F32, name="acc")
+                acc = psum.tile([P, 512], F32, name="bank")
                 mx_pair(acc, ("w", c8 // 4), (c8 % 4) * P, ("x", w))
                 nc.vector.tensor_reduce(
                     out=pooled_v[:, 4 * c8 : 4 * c8 + 4, w, :],
@@ -160,7 +161,7 @@ def tile_hieramaskunitattention_pa_kernel(tc, embeddings, qkv_w, qkv_b, out_0, o
                 )
 
         def q_transposes(c8):
-            bank = tp_pool.tile([P, 512], F32, name="bank")
+            bank = psum.tile([P, 512], F32, name="bank")
             for j in range(4):
                 nc.tensor.transpose(
                     bank[:, j * P : (j + 1) * P],
@@ -202,14 +203,14 @@ def tile_hieramaskunitattention_pa_kernel(tc, embeddings, qkv_w, qkv_b, out_0, o
         load(("x", 0), 4)
         load(("x", 1), 2)
         load(("x", 2), 2)
-        load(("w", 3), 2)
+        load(("w", 3), 1)
         load(("w", 0), 1)
         make_identity(nc, ident[:])
         make_identity(nc, ident_bf[:])
         nc.gpsimd.memset(pooled_v[:, :, 3, :], 0.0)
 
         def spread_bias(n, engine):
-            acc = acc_pool.tile([P, 512], F32, name="acc")
+            acc = psum.tile([P, 512], F32, name="bank")
             nc.tensor.matmul(
                 acc[:], lhsT=ident_bf[:, n : n + 1].to_broadcast([P, P]), rhs=bias_rows[:], start=True, stop=True
             )
@@ -223,54 +224,45 @@ def tile_hieramaskunitattention_pa_kernel(tc, embeddings, qkv_w, qkv_b, out_0, o
             for i in range(len(units)):
                 q_finish(units[i], banks[i], engines[i])
 
-        EARLY = "SVSS"
-        LATE = "SSSS"
-        KV = "VSVS"
-        first, second = (0, 1), (2, 3)
-        prepare_fine(("w", 2), EARLY)
+        ALL = (0, 1, 2, 3)
+        prepare_fine(("w", 2), "SVSV")
         load(("w", 4), 1)
-        prepare_fine(("x", 0), EARLY)
+        prepare_fine(("x", 0), "SVSV")
         load(("w", 5), 1)
         spread_bias(2, "V")
-        spread_bias(3, "S")
-        kv_unit(2, 0, KV, first)
-        prepare_fine(("x", 1), EARLY)
+        kv_unit(2, 0, "VVVS")
+        prepare(("x", 1), "SVSV")
         load(("w", 1), 1)
-        kv_unit(2, 0, KV, second)
-        kv_unit(2, 1, KV, first)
-        prepare_fine(("x", 2), EARLY)
-        kv_unit(2, 1, KV, second)
-        kv_unit(2, 2, KV, first)
-        prepare_fine(("w", 3), EARLY)
+        spread_bias(3, "S")
         spread_bias(4, "V")
+        quantise_whole(("x", 1))
+        prepare(("x", 2), "SVSV")
         spread_bias(5, "S")
-        kv_unit(2, 2, KV, second)
-        kv_unit(3, 0, KV)
-        prepare(("w", 0), LATE)
+        kv_unit(2, 1, "VVVS", ALL, ("x", 2))
+        prepare(("w", 3), "SSSS")
         spread_bias(0, "V")
-        spread_bias(1, "S")
-        kv_unit(3, 1, KV)
-        quantise_whole(("w", 0))
-        prepare(("w", 4), LATE)
-        kv_unit(3, 2, KV)
-        quantise_whole(("w", 4))
+        spread_bias(1, "V")
+        kv_unit(2, 2, "VVVS", ALL, ("w", 3))
+        prepare(("w", 0), "SSSS")
+        kv_unit(3, 0, "VVVS", ALL, ("w", 0))
+        prepare(("w", 4), "SSSS")
+        kv_unit(3, 1, "VVVS", ALL, ("w", 4))
+        prepare(("w", 5), "SSSS")
+        kv_unit(3, 2, "VVVS", ALL, ("w", 5))
+        prepare(("w", 1), "SSSS")
+        kv_unit(4, 0, "VVVS", ALL, ("w", 1))
         q_unit(0)
+        kv_unit(4, 1, "VSVS")
         q_unit(1)
-        kv_unit(4, 0, KV)
+        kv_unit(4, 2, "VSVS")
         q_unit(2)
         finish((0, 1), "SV")
-        prepare(("w", 5), LATE)
-        kv_unit(4, 1, KV)
-        quantise_whole(("w", 5))
+        kv_unit(5, 0, "VSVS")
         q_unit(3)
-        kv_unit(4, 2, KV)
-        finish((2, 3), "SV")
-        prepare(("w", 1), LATE)
-        kv_unit(5, 0, KV)
-        quantise_whole(("w", 1))
-        kv_unit(5, 1, KV)
+        kv_unit(5, 1, "VSVS")
         q_unit(4)
-        kv_unit(5, 2, KV)
+        finish((2, 3), "SV")
+        kv_unit(5, 2, "VSVS")
         q_unit(5)
         q_unit(6)
         finish((4, 5), "SV")

@@ -10,7 +10,6 @@ U8 = mybir.dt.uint8
 FP8X4 = mybir.dt.float8_e4m3fn_x4
 ADD = mybir.AluOpType.add
 MAX = mybir.AluOpType.max
-AXIS_X = mybir.AxisListType.X
 
 P = 128
 FLOPS = 2 * 1536 * 3072 * 1024
@@ -25,9 +24,10 @@ def tile_hieramaskunitattention_pa_kernel(tc, embeddings, qkv_w, qkv_b, out_0, o
     with ExitStack() as ctx:
         const = ctx.enter_context(tc.tile_pool(name="const", bufs=1))
         raw_pool = ctx.enter_context(tc.tile_pool(name="raw", bufs=6))
-        grp_pool = ctx.enter_context(tc.tile_pool(name="grp", bufs=3))
+        grp_w_pool = ctx.enter_context(tc.tile_pool(name="grpw", bufs=2))
+        grp_x_pool = ctx.enter_context(tc.tile_pool(name="grpx", bufs=3))
         code_pool = ctx.enter_context(tc.tile_pool(name="code", bufs=1))
-        out_pool = ctx.enter_context(tc.tile_pool(name="outp", bufs=8))
+        out_pool = ctx.enter_context(tc.tile_pool(name="outp", bufs=7))
         qo_pool = ctx.enter_context(tc.tile_pool(name="qo", bufs=6))
         psum = ctx.enter_context(tc.psum_pool(name="psum", bufs=8))
         if PINNED:
@@ -37,7 +37,6 @@ def tile_hieramaskunitattention_pa_kernel(tc, embeddings, qkv_w, qkv_b, out_0, o
         grouped = {}
         codes = {}
         planes = {}
-        results = {}
 
         def source(key):
             kind, idx = key
@@ -46,7 +45,7 @@ def tile_hieramaskunitattention_pa_kernel(tc, embeddings, qkv_w, qkv_b, out_0, o
             return qkv_w[512 * idx : 512 * idx + 512, :].rearrange("(t p) k -> p t k", p=P)
 
         def load(key, pieces):
-            raw = raw_pool.tile([P, 4096], BF16, name="raw")
+            raw = raw_pool.tile([P, 4096], BF16, name="raw", align_bytes=64)
             raws[key] = raw
             view = raw[:].rearrange("p (t k) -> p t k", t=4)
             src = source(key)
@@ -54,10 +53,16 @@ def tile_hieramaskunitattention_pa_kernel(tc, embeddings, qkv_w, qkv_b, out_0, o
             for a in range(0, 4, step):
                 nc.sync.dma_start(out=view[:, a : a + step, :], in_=src[:, a : a + step, :])
 
-        def begin_group(key):
-            grouped[key] = grp_pool.tile([P, 4096], BF16, name="grouped", align_bytes=64)
+        def new_codes(key):
             codes[key] = code_pool.tile([P, 1024], U32, name="codes_%s%d" % key, align_bytes=64)
             planes[key] = code_pool.tile([P, 1024], U8, name="plane_%s%d" % key, align_bytes=64)
+
+        def begin_group(key):
+            if key[0] == "x":
+                grouped[key] = grp_x_pool.tile([P, 4096], BF16, name="grouped_x", align_bytes=64)
+            else:
+                grouped[key] = grp_w_pool.tile([P, 4096], BF16, name="grouped_w", align_bytes=64)
+            new_codes(key)
 
         def transpose_tile(key, t, engine):
             words = raws[key][:].bitcast(F32)
@@ -86,12 +91,27 @@ def tile_hieramaskunitattention_pa_kernel(tc, embeddings, qkv_w, qkv_b, out_0, o
             for g in range(2):
                 quantise(key, g * 512 + t * P, P)
 
-        def prepare_fine(key, engines):
+        def quantise_whole(key):
+            quantise(key, 0, 1024)
+
+        def spread_bias(n, engine):
+            bank = psum.tile([P, 512], F32, name="bank")
+            nc.tensor.matmul(
+                bank[:], lhsT=ident_bf[:, n : n + 1].to_broadcast([P, P]), rhs=bias_rows[:], start=True, stop=True
+            )
+            if engine == "V":
+                nc.vector.tensor_copy(out=bias[:, n * 512 : (n + 1) * 512], in_=bank[:])
+            else:
+                nc.scalar.copy(out=bias[:, n * 512 : (n + 1) * 512], in_=bank[:])
+
+        def prepare_fine(key, engines, bias_after):
             begin_group(key)
             for t in range(4):
                 transpose_tile(key, t, engines[t])
                 if t > 0:
                     quantise_tile(key, t - 1)
+                for n, engine in bias_after.get(t, ()):
+                    spread_bias(n, engine)
             quantise_tile(key, 3)
 
         def prepare(key, engines):
@@ -99,18 +119,20 @@ def tile_hieramaskunitattention_pa_kernel(tc, embeddings, qkv_w, qkv_b, out_0, o
             for t in range(4):
                 transpose_tile(key, t, engines[t])
 
-        def quantise_halves(key):
-            quantise(key, 0, 512)
-            quantise(key, 512, 512)
+        def reorder_for_q(w):
+            key = ("q", w)
+            grouped[key] = raw_pool.tile([P, 4096], BF16, name="raw", align_bytes=64)
+            new_codes(key)
+            src = grouped[("x", w)][:].bitcast(F32).rearrange("p (c j n u) -> p c n j u", c=2, j=4, n=P, u=2)
+            dst = grouped[key][:].bitcast(F32).rearrange("p (c n j u) -> p c n j u", c=2, n=P, j=4, u=2)
+            for c in range(2):
+                nc.scalar.copy(out=dst[:, c, :, :, :], in_=src[:, c, :, :, :])
 
-        def quantise_whole(key):
-            quantise(key, 0, 1024)
-
-        def mx_pair(acc, stat_key, stat_col, mov_key):
+        def mx_pair(bank, stat_key, stat_col, mov_key):
             for g in range(2):
                 s0 = g * 512 + stat_col
                 nc.tensor.matmul_mx(
-                    out=acc[:],
+                    out=bank[:],
                     lhsT=codes[stat_key][:, s0 : s0 + P].bitcast(FP8X4),
                     lhsT_scale=planes[stat_key][:, s0 : s0 + P],
                     rhs=codes[mov_key][:, g * 512 : (g + 1) * 512].bitcast(FP8X4),
@@ -119,83 +141,58 @@ def tile_hieramaskunitattention_pa_kernel(tc, embeddings, qkv_w, qkv_b, out_0, o
                     stop=(g == 1),
                 )
 
-        def kv_unit(grp, w, engines, tiles=(0, 1, 2, 3), between=None):
+        def kv_unit(grp, w, engines, between=None, after=0):
             dram = out_1 if grp < 4 else out_2
             h0 = 8 * (grp % 2)
-            if (grp, w) not in results:
-                results[(grp, w)] = out_pool.tile([P, 2048], F32, name="res")
-            res = results[(grp, w)]
+            res = out_pool.tile([P, 2048], F32, name="res")
             res_v = res[:].rearrange("p (h j d) -> p h j d", h=8, j=4, d=64)
             bias_v = bias[:, grp * 512 : (grp + 1) * 512].rearrange("p (h d) -> p h d", h=8)
-            accs = {}
-            for j in tiles:
-                acc = psum.tile([P, 512], F32, name="bank")
-                mx_pair(acc, ("x", w), j * P, ("w", grp))
-                accs[j] = acc
-            for j in tiles:
-                acc_v = accs[j][:].rearrange("p (h d) -> p h d", h=8)
-                if engines[j] == "V":
-                    nc.vector.tensor_tensor(out=res_v[:, :, j, :], in0=acc_v, in1=bias_v, op=ADD)
-                else:
-                    nc.scalar.copy(out=res_v[:, :, j, :], in_=acc_v)
-                    nc.gpsimd.tensor_tensor(out=res_v[:, :, j, :], in0=res_v[:, :, j, :], in1=bias_v, op=ADD)
-                if between is not None and j == tiles[0]:
-                    quantise_whole(between)
-            if 3 in tiles:
-                res_h = res[:].rearrange("p (h e) -> p h e", h=8)
-                for a in (0, 4):
-                    nc.sync.dma_start(
-                        out=dram[0, h0 + a : h0 + a + 4, w, :, :].rearrange("h (p j) d -> p h (j d)", j=4),
-                        in_=res_h[:, a : a + 4, :],
-                    )
-
-        def q_unit(c8):
-            for w in range(3):
-                acc = psum.tile([P, 512], F32, name="bank")
-                mx_pair(acc, ("w", c8 // 4), (c8 % 4) * P, ("x", w))
-                nc.vector.tensor_reduce(
-                    out=pooled_v[:, 4 * c8 : 4 * c8 + 4, w, :],
-                    in_=acc[:].rearrange("p (j g q) -> p j q g", j=4, g=4, q=32),
-                    axis=AXIS_X,
-                    op=MAX,
-                )
-
-        def q_transposes(c8):
-            bank = psum.tile([P, 512], F32, name="bank")
+            banks = []
             for j in range(4):
-                nc.tensor.transpose(
-                    bank[:, j * P : (j + 1) * P],
-                    pooled[:, c8 * 512 + j * P : c8 * 512 + (j + 1) * P],
-                    ident[:],
+                bank = psum.tile([P, 512], F32, name="bank")
+                mx_pair(bank, ("x", w), j * P, ("w", grp))
+                banks.append(bank)
+            for j in range(4):
+                bank_v = banks[j][:].rearrange("p (h d) -> p h d", h=8)
+                if engines[j] == "V":
+                    nc.vector.tensor_tensor(out=res_v[:, :, j, :], in0=bank_v, in1=bias_v, op=ADD)
+                else:
+                    nc.scalar.copy(out=res_v[:, :, j, :], in_=bank_v)
+                    nc.gpsimd.tensor_tensor(out=res_v[:, :, j, :], in0=res_v[:, :, j, :], in1=bias_v, op=ADD)
+                if between is not None and j == after:
+                    quantise_whole(between)
+            res_h = res[:].rearrange("p (h e) -> p h e", h=8)
+            for a in (0, 4):
+                nc.sync.dma_start(
+                    out=dram[0, h0 + a : h0 + a + 4, w, :, :].rearrange("h (p j) d -> p h (j d)", j=4),
+                    in_=res_h[:, a : a + 4, :],
                 )
-            return bank
 
-        def q_finish(c8, bank, engine):
-            qo = qo_pool.tile([P, 512], F32, name="qo")
-            qo_v = qo[0:96, :].rearrange("p (h j d) -> p h j d", h=2, j=4, d=64)
-            bank_v = bank[0:96, :].rearrange("p (j h d) -> p h j d", j=4, h=2, d=64)
-            bias_v = (
-                bias[0:96, c8 * P : (c8 + 1) * P]
-                .rearrange("p (h d) -> p h d", h=2)
-                .unsqueeze(2)
-                .to_broadcast([96, 2, 4, 64])
-            )
-            if engine == "V":
-                nc.vector.tensor_tensor(out=qo_v, in0=bank_v, in1=bias_v, op=ADD)
+        def q_unit(w, grp, add_engine):
+            best = qo_pool.tile([P, 512], F32, name="best")
+            for g in range(4):
+                bank = psum.tile([P, 512], F32, name="bank")
+                mx_pair(bank, ("q", w), g * P, ("w", grp))
+                if g == 0:
+                    nc.scalar.copy(out=best[:], in_=bank[:])
+                else:
+                    nc.vector.tensor_tensor(out=best[:], in0=bank[:], in1=best[:], op=MAX)
+            bias_q = bias[:, grp * 512 : (grp + 1) * 512]
+            if add_engine == "V":
+                nc.vector.tensor_tensor(out=best[:], in0=best[:], in1=bias_q, op=ADD)
             else:
-                nc.scalar.copy(out=qo_v, in_=bank_v)
-                nc.gpsimd.tensor_tensor(out=qo_v, in0=qo_v, in1=bias_v, op=ADD)
-            nc.sync.dma_start(
-                out=out_0[0, 2 * c8 : 2 * c8 + 2, :, :, :].rearrange("h w (q j) d -> (w q) h (j d)", j=4),
-                in_=qo[0:96, :].rearrange("p (h e) -> p h e", h=2),
-            )
+                nc.gpsimd.tensor_tensor(out=best[:], in0=best[:], in1=bias_q, op=ADD)
+            best_h = best[:].rearrange("p (h d) -> p h d", h=8)
+            for a in (0, 4):
+                nc.sync.dma_start(
+                    out=out_0[0, 8 * grp + a : 8 * grp + a + 4, w, :, :].rearrange("h i d -> i h d"),
+                    in_=best_h[:, a : a + 4, :],
+                )
 
         bias_rows = const.tile([P, 512], BF16, name="bias_rows")
         ident_bf = const.tile([P, P], BF16, name="ident_bf")
         ident = const.tile([P, P], F32, name="ident")
         bias = const.tile([P, 3072], F32, name="bias")
-        pooled = const.tile([P, 4096], F32, name="pooled")
-        pooled_v = pooled[:].rearrange("p (a s q) -> p a s q", a=32, s=4, q=32)
 
         nc.vector.memset(bias_rows[:], 0.0)
         nc.scalar.dma_start(out=bias_rows[0:6, :], in_=qkv_b.rearrange("(n c) -> n c", n=6))
@@ -204,67 +201,43 @@ def tile_hieramaskunitattention_pa_kernel(tc, embeddings, qkv_w, qkv_b, out_0, o
         load(("x", 1), 2)
         load(("x", 2), 2)
         load(("w", 3), 1)
-        load(("w", 0), 1)
-        make_identity(nc, ident[:])
-        make_identity(nc, ident_bf[:])
-        nc.gpsimd.memset(pooled_v[:, :, 3, :], 0.0)
-
-        def spread_bias(n, engine):
-            acc = psum.tile([P, 512], F32, name="bank")
-            nc.tensor.matmul(
-                acc[:], lhsT=ident_bf[:, n : n + 1].to_broadcast([P, P]), rhs=bias_rows[:], start=True, stop=True
-            )
-            if engine == "V":
-                nc.vector.tensor_copy(out=bias[:, n * 512 : (n + 1) * 512], in_=acc[:])
-            else:
-                nc.scalar.copy(out=bias[:, n * 512 : (n + 1) * 512], in_=acc[:])
-
-        def finish(units, engines):
-            banks = [q_transposes(c8) for c8 in units]
-            for i in range(len(units)):
-                q_finish(units[i], banks[i], engines[i])
-
-        ALL = (0, 1, 2, 3)
-        prepare_fine(("w", 2), "SVSV")
         load(("w", 4), 1)
-        prepare_fine(("x", 0), "SVSV")
-        load(("w", 5), 1)
+        make_identity(nc, ident_bf[:])
+        make_identity(nc, ident[:])
+
         spread_bias(2, "V")
+        spread_bias(3, "S")
+        prepare_fine(("w", 2), "SVSV", {1: ((4, "S"), (5, "V"))})
+        load(("w", 5), 1)
+        prepare_fine(("x", 0), "SSVS", {0: ((0, "S"), (1, "S"))})
+        load(("w", 0), 1)
         kv_unit(2, 0, "VVVS")
         prepare(("x", 1), "SVSV")
         load(("w", 1), 1)
-        spread_bias(3, "S")
-        spread_bias(4, "V")
         quantise_whole(("x", 1))
         prepare(("x", 2), "SVSV")
-        spread_bias(5, "S")
-        kv_unit(2, 1, "VVVS", ALL, ("x", 2))
+        kv_unit(2, 1, "VVVS", ("x", 2))
         prepare(("w", 3), "SSSS")
-        spread_bias(0, "V")
-        spread_bias(1, "V")
-        kv_unit(2, 2, "VVVS", ALL, ("w", 3))
-        prepare(("w", 0), "SSSS")
-        kv_unit(3, 0, "VVVS", ALL, ("w", 0))
+        kv_unit(2, 2, "VVVS", ("w", 3))
         prepare(("w", 4), "SSSS")
-        kv_unit(3, 1, "VVVS", ALL, ("w", 4))
+        kv_unit(3, 0, "VVVS", ("w", 4))
         prepare(("w", 5), "SSSS")
-        kv_unit(3, 2, "VVVS", ALL, ("w", 5))
+        kv_unit(3, 1, "VVVS", ("w", 5))
+        prepare(("w", 0), "SSSS")
+        kv_unit(3, 2, "VVVS", ("w", 0))
         prepare(("w", 1), "SSSS")
-        kv_unit(4, 0, "VVVS", ALL, ("w", 1))
-        q_unit(0)
-        kv_unit(4, 1, "VSVS")
-        q_unit(1)
-        kv_unit(4, 2, "VSVS")
-        q_unit(2)
-        finish((0, 1), "SV")
-        kv_unit(5, 0, "VSVS")
-        q_unit(3)
+        kv_unit(4, 0, "VVVS", ("w", 1))
+        reorder_for_q(0)
+        kv_unit(4, 1, "VVVS", ("q", 0), 2)
+        reorder_for_q(1)
+        kv_unit(4, 2, "VVVS", ("q", 1), 2)
+        reorder_for_q(2)
+        kv_unit(5, 0, "VVVS", ("q", 2), 2)
+        q_unit(0, 0, "G")
         kv_unit(5, 1, "VSVS")
-        q_unit(4)
-        finish((2, 3), "SV")
+        q_unit(1, 0, "G")
         kv_unit(5, 2, "VSVS")
-        q_unit(5)
-        q_unit(6)
-        finish((4, 5), "SV")
-        q_unit(7)
-        finish((6, 7), "VV")
+        q_unit(2, 0, "G")
+        q_unit(0, 1, "G")
+        q_unit(1, 1, "G")
+        q_unit(2, 1, "V")

@@ -37,6 +37,7 @@ def tile_hieramaskunitattention_pa_kernel(tc, embeddings, qkv_w, qkv_b, out_0, o
         grouped = {}
         codes = {}
         planes = {}
+        results = {}
 
         def source(key):
             kind, idx = key
@@ -44,13 +45,13 @@ def tile_hieramaskunitattention_pa_kernel(tc, embeddings, qkv_w, qkv_b, out_0, o
                 return x_rows[idx]
             return qkv_w[512 * idx : 512 * idx + 512, :].rearrange("(t p) k -> p t k", p=P)
 
-        def load(key, pieces):
-            raw = raw_pool.tile([P, 4096], BF16, name="raw", align_bytes=64)
-            raws[key] = raw
-            view = raw[:].rearrange("p (t k) -> p t k", t=4)
+        def load(key, pieces, first=0, last=4):
+            if key not in raws:
+                raws[key] = raw_pool.tile([P, 4096], BF16, name="raw", align_bytes=64)
+            view = raws[key][:].rearrange("p (t k) -> p t k", t=4)
             src = source(key)
             step = 4 // pieces
-            for a in range(0, 4, step):
+            for a in range(first, last, step):
                 nc.sync.dma_start(out=view[:, a : a + step, :], in_=src[:, a : a + step, :])
 
         def new_codes(key):
@@ -128,31 +129,34 @@ def tile_hieramaskunitattention_pa_kernel(tc, embeddings, qkv_w, qkv_b, out_0, o
             for c in range(2):
                 nc.scalar.copy(out=dst[:, c, :, :, :], in_=src[:, c, :, :, :])
 
-        def mx_pair(bank, stat_key, stat_col, mov_key):
+        def mx_pair(bank, stat_key, stat_col, mov_key, mov_col=0, width=512):
             for g in range(2):
                 s0 = g * 512 + stat_col
+                m0 = g * 512 + mov_col
                 nc.tensor.matmul_mx(
-                    out=bank[:],
+                    out=bank[:, 0:width],
                     lhsT=codes[stat_key][:, s0 : s0 + P].bitcast(FP8X4),
                     lhsT_scale=planes[stat_key][:, s0 : s0 + P],
-                    rhs=codes[mov_key][:, g * 512 : (g + 1) * 512].bitcast(FP8X4),
-                    rhs_scale=planes[mov_key][:, g * 512 : (g + 1) * 512],
+                    rhs=codes[mov_key][:, m0 : m0 + width].bitcast(FP8X4),
+                    rhs_scale=planes[mov_key][:, m0 : m0 + width],
                     start=(g == 0),
                     stop=(g == 1),
                 )
 
-        def kv_unit(grp, w, engines, between=None, after=0):
+        def kv_unit(grp, w, engines, between=None, after=0, tiles=(0, 1, 2, 3)):
             dram = out_1 if grp < 4 else out_2
             h0 = 8 * (grp % 2)
-            res = out_pool.tile([P, 2048], F32, name="res")
+            if (grp, w) not in results:
+                results[(grp, w)] = out_pool.tile([P, 2048], F32, name="res")
+            res = results[(grp, w)]
             res_v = res[:].rearrange("p (h j d) -> p h j d", h=8, j=4, d=64)
             bias_v = bias[:, grp * 512 : (grp + 1) * 512].rearrange("p (h d) -> p h d", h=8)
-            banks = []
-            for j in range(4):
+            banks = {}
+            for j in tiles:
                 bank = psum.tile([P, 512], F32, name="bank")
                 mx_pair(bank, ("x", w), j * P, ("w", grp))
-                banks.append(bank)
-            for j in range(4):
+                banks[j] = bank
+            for j in tiles:
                 bank_v = banks[j][:].rearrange("p (h d) -> p h d", h=8)
                 if engines[j] == "V":
                     nc.vector.tensor_tensor(out=res_v[:, :, j, :], in0=bank_v, in1=bias_v, op=ADD)
@@ -161,6 +165,8 @@ def tile_hieramaskunitattention_pa_kernel(tc, embeddings, qkv_w, qkv_b, out_0, o
                     nc.gpsimd.tensor_tensor(out=res_v[:, :, j, :], in0=res_v[:, :, j, :], in1=bias_v, op=ADD)
                 if between is not None and j == after:
                     quantise_whole(between)
+            if 3 not in tiles:
+                return
             res_h = res[:].rearrange("p (h e) -> p h e", h=8)
             for a in (0, 4):
                 nc.sync.dma_start(
@@ -168,24 +174,25 @@ def tile_hieramaskunitattention_pa_kernel(tc, embeddings, qkv_w, qkv_b, out_0, o
                     in_=res_h[:, a : a + 4, :],
                 )
 
-        def q_unit(w, grp, add_engine):
+        def q_unit(w, grp, add_engine, col=0, width=512):
             best = qo_pool.tile([P, 512], F32, name="best")
             for g in range(4):
                 bank = psum.tile([P, 512], F32, name="bank")
-                mx_pair(bank, ("q", w), g * P, ("w", grp))
+                mx_pair(bank, ("q", w), g * P, ("w", grp), col, width)
                 if g == 0:
-                    nc.scalar.copy(out=best[:], in_=bank[:])
+                    nc.scalar.copy(out=best[:, 0:width], in_=bank[:, 0:width])
                 else:
-                    nc.vector.tensor_tensor(out=best[:], in0=bank[:], in1=best[:], op=MAX)
-            bias_q = bias[:, grp * 512 : (grp + 1) * 512]
+                    nc.vector.tensor_tensor(out=best[:, 0:width], in0=bank[:, 0:width], in1=best[:, 0:width], op=MAX)
+            bias_q = bias[:, grp * 512 + col : grp * 512 + col + width]
             if add_engine == "V":
-                nc.vector.tensor_tensor(out=best[:], in0=best[:], in1=bias_q, op=ADD)
+                nc.vector.tensor_tensor(out=best[:, 0:width], in0=best[:, 0:width], in1=bias_q, op=ADD)
             else:
-                nc.gpsimd.tensor_tensor(out=best[:], in0=best[:], in1=bias_q, op=ADD)
+                nc.gpsimd.tensor_tensor(out=best[:, 0:width], in0=best[:, 0:width], in1=bias_q, op=ADD)
             best_h = best[:].rearrange("p (h d) -> p h d", h=8)
-            for a in (0, 4):
+            h0 = 8 * grp + col // 64
+            for a in range(0, width // 64, 4):
                 nc.sync.dma_start(
-                    out=out_0[0, 8 * grp + a : 8 * grp + a + 4, w, :, :].rearrange("h i d -> i h d"),
+                    out=out_0[0, h0 + a : h0 + a + 4, w, :, :].rearrange("h i d -> i h d"),
                     in_=best_h[:, a : a + 4, :],
                 )
 
@@ -194,9 +201,12 @@ def tile_hieramaskunitattention_pa_kernel(tc, embeddings, qkv_w, qkv_b, out_0, o
         ident = const.tile([P, P], F32, name="ident")
         bias = const.tile([P, 3072], F32, name="bias")
 
+        zeros = const.tile([P, 512], BF16, name="zeros")
         nc.vector.memset(bias_rows[:], 0.0)
-        nc.scalar.dma_start(out=bias_rows[0:6, :], in_=qkv_b.rearrange("(n c) -> n c", n=6))
-        load(("w", 2), 4)
+        nc.vector.memset(zeros[:], 0.0)
+        load(("w", 2), 4, 0, 2)
+        nc.sync.dma_start(out=bias_rows[0:6, :], in_=qkv_b.rearrange("(n c) -> n c", n=6))
+        load(("w", 2), 4, 2, 4)
         load(("x", 0), 4)
         load(("x", 1), 2)
         load(("x", 2), 2)
@@ -205,15 +215,17 @@ def tile_hieramaskunitattention_pa_kernel(tc, embeddings, qkv_w, qkv_b, out_0, o
         make_identity(nc, ident_bf[:])
         make_identity(nc, ident[:])
 
-        spread_bias(2, "V")
-        spread_bias(3, "S")
-        prepare_fine(("w", 2), "SVSV", {1: ((4, "S"), (5, "V"))})
+        warm = psum.tile([P, 512], F32, name="bank")
+        for i in range(4):
+            nc.tensor.matmul(warm[:], lhsT=ident_bf[:], rhs=zeros[:], start=True, stop=True)
+        prepare_fine(("w", 2), "SVSV", {1: ((2, "V"), (3, "S")), 3: ((4, "S"), (5, "V"))})
         load(("w", 5), 1)
-        prepare_fine(("x", 0), "SSVS", {0: ((0, "S"), (1, "S"))})
+        prepare_fine(("x", 0), "SSVS", {1: ((0, "S"), (1, "S"))})
         load(("w", 0), 1)
-        kv_unit(2, 0, "VVVS")
+        kv_unit(2, 0, "VVVV", tiles=(0, 1))
         prepare(("x", 1), "SVSV")
         load(("w", 1), 1)
+        kv_unit(2, 0, "VVVV", tiles=(2, 3))
         quantise_whole(("x", 1))
         prepare(("x", 2), "SVSV")
         kv_unit(2, 1, "VVVS", ("x", 2))
@@ -240,4 +252,5 @@ def tile_hieramaskunitattention_pa_kernel(tc, embeddings, qkv_w, qkv_b, out_0, o
         q_unit(2, 0, "G")
         q_unit(0, 1, "G")
         q_unit(1, 1, "G")
-        q_unit(2, 1, "V")
+        q_unit(2, 1, "G", 0, 256)
+        q_unit(2, 1, "V", 256, 256)

@@ -7,6 +7,7 @@ F32 = mybir.dt.float32
 BF16 = mybir.dt.bfloat16
 U32 = mybir.dt.uint32
 U8 = mybir.dt.uint8
+I32 = mybir.dt.int32
 FP8X4 = mybir.dt.float8_e4m3fn_x4
 ADD = mybir.AluOpType.add
 MAX = mybir.AluOpType.max
@@ -57,6 +58,8 @@ def tile_hieramaskunitattention_pa_kernel(tc, embeddings, qkv_w, qkv_b, out_0, o
         def new_codes(key):
             codes[key] = code_pool.tile([P, 1024], U32, name="codes_%s%d" % key, align_bytes=64)
             planes[key] = code_pool.tile([P, 1024], U8, name="plane_%s%d" % key, align_bytes=64)
+            if key[0] == "x":
+                nc.gpsimd.memset(planes[key][:].bitcast(U32), 0)
 
         def begin_group(key):
             if key[0] == "x":
@@ -74,7 +77,11 @@ def tile_hieramaskunitattention_pa_kernel(tc, embeddings, qkv_w, qkv_b, out_0, o
                     words[:, t * 512 + gu * P : t * 512 + (gu + 1) * P],
                     ident[:],
                 )
-            dst = grouped[key][:].bitcast(F32).rearrange("p (g t n u) -> p g t n u", g=2, t=4, n=P, u=2)
+            words_out = grouped[key][:].bitcast(F32)
+            if key[0] == "x":
+                dst = words_out.rearrange("p (t g n u) -> p g t n u", g=2, t=4, n=P, u=2)
+            else:
+                dst = words_out.rearrange("p (g t n u) -> p g t n u", g=2, t=4, n=P, u=2)
             src = bank[:].rearrange("p (g u n) -> p g n u", g=2, u=2, n=P)
             if engine == "S":
                 nc.scalar.copy(out=dst[:, :, t, :, :], in_=src)
@@ -89,8 +96,11 @@ def tile_hieramaskunitattention_pa_kernel(tc, embeddings, qkv_w, qkv_b, out_0, o
             )
 
         def quantise_tile(key, t):
-            for g in range(2):
-                quantise(key, g * 512 + t * P, P)
+            if key[0] == "x":
+                quantise(key, t * 256, 256)
+            else:
+                for g in range(2):
+                    quantise(key, g * 512 + t * P, P)
 
         def quantise_whole(key):
             quantise(key, 0, 1024)
@@ -122,16 +132,16 @@ def tile_hieramaskunitattention_pa_kernel(tc, embeddings, qkv_w, qkv_b, out_0, o
 
         def reorder_for_q(w):
             key = ("q", w)
-            grouped[key] = raw_pool.tile([P, 4096], BF16, name="raw", align_bytes=64)
             new_codes(key)
-            src = grouped[("x", w)][:].bitcast(F32).rearrange("p (c j n u) -> p c n j u", c=2, j=4, n=P, u=2)
-            dst = grouped[key][:].bitcast(F32).rearrange("p (c n j u) -> p c n j u", c=2, n=P, j=4, u=2)
-            for c in range(2):
-                nc.scalar.copy(out=dst[:, c, :, :, :], in_=src[:, c, :, :, :])
+            for table, dtype in ((codes, I32), (planes, U8)):
+                nc.vector.tensor_copy(
+                    out=table[key][:].bitcast(dtype).rearrange("p (c t) -> p c t", t=4),
+                    in_=table[("x", w)][:].bitcast(dtype).rearrange("p (t c) -> p c t", t=4),
+                )
 
-        def mx_pair(bank, stat_key, stat_col, mov_key, mov_col=0, width=512):
+        def mx_pair(bank, stat_key, stat, mov_key, mov_col=0, width=512):
             for g in range(2):
-                s0 = g * 512 + stat_col
+                s0 = (2 * stat + g) * P if stat_key[0] == "x" else (4 * g + stat) * P
                 m0 = g * 512 + mov_col
                 nc.tensor.matmul_mx(
                     out=bank[:, 0:width],
@@ -154,7 +164,7 @@ def tile_hieramaskunitattention_pa_kernel(tc, embeddings, qkv_w, qkv_b, out_0, o
             banks = {}
             for j in tiles:
                 bank = psum.tile([P, 512], F32, name="bank")
-                mx_pair(bank, ("x", w), j * P, ("w", grp))
+                mx_pair(bank, ("x", w), j, ("w", grp))
                 banks[j] = bank
             for j in tiles:
                 bank_v = banks[j][:].rearrange("p (h d) -> p h d", h=8)
@@ -164,7 +174,10 @@ def tile_hieramaskunitattention_pa_kernel(tc, embeddings, qkv_w, qkv_b, out_0, o
                     nc.scalar.copy(out=res_v[:, :, j, :], in_=bank_v)
                     nc.gpsimd.tensor_tensor(out=res_v[:, :, j, :], in0=res_v[:, :, j, :], in1=bias_v, op=ADD)
                 if between is not None and j == after:
-                    quantise_whole(between)
+                    if between[0] == "q":
+                        reorder_for_q(between[1])
+                    else:
+                        quantise_whole(between)
             if 3 not in tiles:
                 return
             res_h = res[:].rearrange("p (h e) -> p h e", h=8)
@@ -178,7 +191,7 @@ def tile_hieramaskunitattention_pa_kernel(tc, embeddings, qkv_w, qkv_b, out_0, o
             best = qo_pool.tile([P, 512], F32, name="best")
             for g in range(4):
                 bank = psum.tile([P, 512], F32, name="bank")
-                mx_pair(bank, ("q", w), g * P, ("w", grp), col, width)
+                mx_pair(bank, ("q", w), g, ("w", grp), col, width)
                 if g == 0:
                     nc.scalar.copy(out=best[:, 0:width], in_=bank[:, 0:width])
                 else:
@@ -239,11 +252,8 @@ def tile_hieramaskunitattention_pa_kernel(tc, embeddings, qkv_w, qkv_b, out_0, o
         kv_unit(3, 2, "VVVS", ("w", 0))
         prepare(("w", 1), "SSSS")
         kv_unit(4, 0, "VVVS", ("w", 1))
-        reorder_for_q(0)
         kv_unit(4, 1, "VVVS", ("q", 0), 2)
-        reorder_for_q(1)
         kv_unit(4, 2, "VVVS", ("q", 1), 2)
-        reorder_for_q(2)
         kv_unit(5, 0, "VVVS", ("q", 2), 2)
         q_unit(0, 0, "G")
         kv_unit(5, 1, "VSVS")

@@ -6,16 +6,14 @@ from concourse.masks import make_identity
 F32 = mybir.dt.float32
 BF16 = mybir.dt.bfloat16
 U32 = mybir.dt.uint32
-U8 = mybir.dt.uint8
 I32 = mybir.dt.int32
+U8 = mybir.dt.uint8
 FP8X4 = mybir.dt.float8_e4m3fn_x4
 ADD = mybir.AluOpType.add
 MAX = mybir.AluOpType.max
 
 P = 128
 FLOPS = 2 * 1536 * 3072 * 1024
-
-PINNED = True
 
 
 def tile_hieramaskunitattention_pa_kernel(tc, embeddings, qkv_w, qkv_b, out_0, out_1, out_2):
@@ -24,33 +22,31 @@ def tile_hieramaskunitattention_pa_kernel(tc, embeddings, qkv_w, qkv_b, out_0, o
 
     with ExitStack() as ctx:
         const = ctx.enter_context(tc.tile_pool(name="const", bufs=1))
-        raw_pool = ctx.enter_context(tc.tile_pool(name="raw", bufs=6))
+        raw_pool = ctx.enter_context(tc.tile_pool(name="raw", bufs=9))
         grp_w_pool = ctx.enter_context(tc.tile_pool(name="grpw", bufs=2))
         grp_x_pool = ctx.enter_context(tc.tile_pool(name="grpx", bufs=3))
         code_pool = ctx.enter_context(tc.tile_pool(name="code", bufs=1))
-        out_pool = ctx.enter_context(tc.tile_pool(name="outp", bufs=7))
+        out_pool = ctx.enter_context(tc.tile_pool(name="outp", bufs=6))
         qo_pool = ctx.enter_context(tc.tile_pool(name="qo", bufs=6))
         psum = ctx.enter_context(tc.psum_pool(name="psum", bufs=8))
-        if PINNED:
-            ctx.enter_context(tc.manual_schedule())
+        ctx.enter_context(tc.manual_schedule())
 
         raws = {}
         grouped = {}
         codes = {}
         planes = {}
+        banks = {}
         results = {}
 
-        def source(key):
-            kind, idx = key
-            if kind == "x":
-                return x_rows[idx]
-            return qkv_w[512 * idx : 512 * idx + 512, :].rearrange("(t p) k -> p t k", p=P)
-
         def load(key, pieces, first=0, last=4):
+            kind, idx = key
             if key not in raws:
                 raws[key] = raw_pool.tile([P, 4096], BF16, name="raw", align_bytes=64)
             view = raws[key][:].rearrange("p (t k) -> p t k", t=4)
-            src = source(key)
+            if kind == "x":
+                src = x_rows[idx]
+            else:
+                src = qkv_w[512 * idx : 512 * idx + 512, :].rearrange("(t p) k -> p t k", p=P)
             step = 4 // pieces
             for a in range(first, last, step):
                 nc.sync.dma_start(out=view[:, a : a + step, :], in_=src[:, a : a + step, :])
@@ -61,14 +57,23 @@ def tile_hieramaskunitattention_pa_kernel(tc, embeddings, qkv_w, qkv_b, out_0, o
             if key[0] == "x":
                 nc.gpsimd.memset(planes[key][:].bitcast(U32), 0)
 
-        def begin_group(key):
-            if key[0] == "x":
-                grouped[key] = grp_x_pool.tile([P, 4096], BF16, name="grouped_x", align_bytes=64)
+        def copy_out(engine, out, in_):
+            if engine == "S":
+                nc.scalar.copy(out=out, in_=in_)
             else:
-                grouped[key] = grp_w_pool.tile([P, 4096], BF16, name="grouped_w", align_bytes=64)
-            new_codes(key)
+                nc.vector.tensor_copy(out=out, in_=in_)
 
         def transpose_tile(key, t, engine):
+            if key[0] == "x":
+                if t % 2 == 0:
+                    grouped[key + (t // 2,)] = grp_x_pool.tile([P, 2048], BF16, name="grouped_x", align_bytes=64)
+                dst = grouped[key + (t // 2,)][:].bitcast(F32)
+                dst = dst.rearrange("p (t g n u) -> p t g n u", t=2, g=2, n=P, u=2)[:, t % 2, :, :, :]
+            else:
+                if t == 0:
+                    grouped[key] = grp_w_pool.tile([P, 4096], BF16, name="grouped_w", align_bytes=64)
+                dst = grouped[key][:].bitcast(F32)
+                dst = dst.rearrange("p (g t n u) -> p g t n u", g=2, t=4, n=P, u=2)[:, :, t, :, :]
             words = raws[key][:].bitcast(F32)
             bank = psum.tile([P, 512], F32, name="bank")
             for gu in range(4):
@@ -77,67 +82,47 @@ def tile_hieramaskunitattention_pa_kernel(tc, embeddings, qkv_w, qkv_b, out_0, o
                     words[:, t * 512 + gu * P : t * 512 + (gu + 1) * P],
                     ident[:],
                 )
-            words_out = grouped[key][:].bitcast(F32)
-            if key[0] == "x":
-                dst = words_out.rearrange("p (t g n u) -> p g t n u", g=2, t=4, n=P, u=2)
-            else:
-                dst = words_out.rearrange("p (g t n u) -> p g t n u", g=2, t=4, n=P, u=2)
-            src = bank[:].rearrange("p (g u n) -> p g n u", g=2, u=2, n=P)
-            if engine == "S":
-                nc.scalar.copy(out=dst[:, :, t, :, :], in_=src)
-            else:
-                nc.vector.tensor_copy(out=dst[:, :, t, :, :], in_=src)
+            copy_out(engine, dst, bank[:].rearrange("p (g u n) -> p g n u", g=2, u=2, n=P))
 
-        def quantise(key, first, width):
+        def quantise(key, first, width, source):
             nc.vector.quantize_mx(
                 out=codes[key][:, first : first + width].bitcast(FP8X4),
                 scales=planes[key][:, first : first + width],
-                in_=grouped[key][:, 4 * first : 4 * (first + width)],
+                in_=source,
             )
 
-        def quantise_tile(key, t):
-            if key[0] == "x":
-                quantise(key, t * 256, 256)
-            else:
-                for g in range(2):
-                    quantise(key, g * 512 + t * P, P)
+        def quantise_w(idx):
+            key = ("w", idx)
+            quantise(key, 0, 1024, grouped[key][:])
 
-        def quantise_whole(key):
-            quantise(key, 0, 1024)
+        def quantise_w_half(idx, half):
+            key = ("w", idx)
+            for g in range(2):
+                a = 512 * g + 256 * half
+                quantise(key, a, 256, grouped[key][:, 4 * a : 4 * a + 1024])
+
+        def quantise_x_pair(w, pair):
+            key = ("x", w)
+            quantise(key, 512 * pair, 512, grouped[key + (pair,)][:])
+
+        def quantise_x_tile(w, t):
+            key = ("x", w)
+            a = 1024 * (t % 2)
+            quantise(key, 256 * t, 256, grouped[key + (t // 2,)][:, a : a + 1024])
+
+        def move_for_q(w):
+            for table, dtype in ((codes, I32), (planes, U8)):
+                nc.vector.tensor_copy(
+                    out=table[("q", w)][:].bitcast(dtype).rearrange("p (c t) -> p c t", t=4),
+                    in_=table[("x", w)][:].bitcast(dtype).rearrange("p (t c) -> p c t", t=4),
+                )
 
         def spread_bias(n, engine):
             bank = psum.tile([P, 512], F32, name="bank")
             nc.tensor.matmul(
                 bank[:], lhsT=ident_bf[:, n : n + 1].to_broadcast([P, P]), rhs=bias_rows[:], start=True, stop=True
             )
-            if engine == "V":
-                nc.vector.tensor_copy(out=bias[:, n * 512 : (n + 1) * 512], in_=bank[:])
-            else:
-                nc.scalar.copy(out=bias[:, n * 512 : (n + 1) * 512], in_=bank[:])
-
-        def prepare_fine(key, engines, bias_after):
-            begin_group(key)
-            for t in range(4):
-                transpose_tile(key, t, engines[t])
-                if t > 0:
-                    quantise_tile(key, t - 1)
-                for n, engine in bias_after.get(t, ()):
-                    spread_bias(n, engine)
-            quantise_tile(key, 3)
-
-        def prepare(key, engines):
-            begin_group(key)
-            for t in range(4):
-                transpose_tile(key, t, engines[t])
-
-        def reorder_for_q(w):
-            key = ("q", w)
-            new_codes(key)
-            for table, dtype in ((codes, I32), (planes, U8)):
-                nc.vector.tensor_copy(
-                    out=table[key][:].bitcast(dtype).rearrange("p (c t) -> p c t", t=4),
-                    in_=table[("x", w)][:].bitcast(dtype).rearrange("p (t c) -> p c t", t=4),
-                )
+            copy_out(engine, bias[:, n * 512 : (n + 1) * 512], bank[:])
 
         def mx_pair(bank, stat_key, stat, mov_key, mov_col=0, width=512):
             for g in range(2):
@@ -153,114 +138,153 @@ def tile_hieramaskunitattention_pa_kernel(tc, embeddings, qkv_w, qkv_b, out_0, o
                     stop=(g == 1),
                 )
 
-        def kv_unit(grp, w, engines, between=None, after=0, tiles=(0, 1, 2, 3)):
-            dram = out_1 if grp < 4 else out_2
-            h0 = 8 * (grp % 2)
-            if (grp, w) not in results:
+        def kv_matmul(grp, w, j):
+            bank = psum.tile([P, 512], F32, name="bank")
+            mx_pair(bank, ("x", w), j, ("w", grp))
+            banks[(grp, w, j)] = bank
+
+        def kv_finish(grp, w, j, engine):
+            if j == 0:
                 results[(grp, w)] = out_pool.tile([P, 2048], F32, name="res")
             res = results[(grp, w)]
-            res_v = res[:].rearrange("p (h j d) -> p h j d", h=8, j=4, d=64)
+            part = res[:].rearrange("p (h j d) -> p h j d", h=8, j=4, d=64)[:, :, j, :]
+            bank_v = banks[(grp, w, j)][:].rearrange("p (h d) -> p h d", h=8)
             bias_v = bias[:, grp * 512 : (grp + 1) * 512].rearrange("p (h d) -> p h d", h=8)
-            banks = {}
-            for j in tiles:
-                bank = psum.tile([P, 512], F32, name="bank")
-                mx_pair(bank, ("x", w), j, ("w", grp))
-                banks[j] = bank
-            for j in tiles:
-                bank_v = banks[j][:].rearrange("p (h d) -> p h d", h=8)
-                if engines[j] == "V":
-                    nc.vector.tensor_tensor(out=res_v[:, :, j, :], in0=bank_v, in1=bias_v, op=ADD)
-                else:
-                    nc.scalar.copy(out=res_v[:, :, j, :], in_=bank_v)
-                    nc.gpsimd.tensor_tensor(out=res_v[:, :, j, :], in0=res_v[:, :, j, :], in1=bias_v, op=ADD)
-                if between is not None and j == after:
-                    if between[0] == "q":
-                        reorder_for_q(between[1])
-                    else:
-                        quantise_whole(between)
-            if 3 not in tiles:
-                return
-            res_h = res[:].rearrange("p (h e) -> p h e", h=8)
-            for a in (0, 4):
-                nc.sync.dma_start(
-                    out=dram[0, h0 + a : h0 + a + 4, w, :, :].rearrange("h (p j) d -> p h (j d)", j=4),
-                    in_=res_h[:, a : a + 4, :],
-                )
-
-        def q_unit(w, grp, add_engine, col=0, width=512):
-            best = qo_pool.tile([P, 512], F32, name="best")
-            for g in range(4):
-                bank = psum.tile([P, 512], F32, name="bank")
-                mx_pair(bank, ("q", w), g, ("w", grp), col, width)
-                if g == 0:
-                    nc.scalar.copy(out=best[:, 0:width], in_=bank[:, 0:width])
-                else:
-                    nc.vector.tensor_tensor(out=best[:, 0:width], in0=bank[:, 0:width], in1=best[:, 0:width], op=MAX)
-            bias_q = bias[:, grp * 512 + col : grp * 512 + col + width]
-            if add_engine == "V":
-                nc.vector.tensor_tensor(out=best[:, 0:width], in0=best[:, 0:width], in1=bias_q, op=ADD)
+            if engine == "V":
+                nc.vector.tensor_tensor(out=part, in0=bank_v, in1=bias_v, op=ADD)
             else:
-                nc.gpsimd.tensor_tensor(out=best[:, 0:width], in0=best[:, 0:width], in1=bias_q, op=ADD)
-            best_h = best[:].rearrange("p (h d) -> p h d", h=8)
-            h0 = 8 * grp + col // 64
-            for a in range(0, width // 64, 4):
+                nc.scalar.copy(out=part, in_=bank_v)
+                nc.gpsimd.tensor_tensor(out=part, in0=part, in1=bias_v, op=ADD)
+            if j == 3:
+                dram = out_1 if grp < 4 else out_2
+                h0 = 8 * (grp % 2)
+                res_h = res[:].rearrange("p (h e) -> p h e", h=8)
+                for a in (0, 4):
+                    nc.sync.dma_start(
+                        out=dram[0, h0 + a : h0 + a + 4, w, :, :].rearrange("h (p j) d -> p h (j d)", j=4),
+                        in_=res_h[:, a : a + 4, :],
+                    )
+
+        def kv_unit(grp, w, engines, between=None):
+            for j in range(4):
+                kv_matmul(grp, w, j)
+            for j in range(4):
+                kv_finish(grp, w, j, engines[j])
+                if between is not None and j == 0:
+                    between()
+
+        def q_units(units, add_engine):
+            best = [qo_pool.tile([P, 512], F32, name="best") for unit in units]
+            for g in range(4):
+                for (w, grp, col, width), top in zip(units, best):
+                    bank = psum.tile([P, 512], F32, name="bank")
+                    mx_pair(bank, ("q", w), g, ("w", grp), col, width)
+                    if g == 0:
+                        nc.scalar.copy(out=top[:, 0:width], in_=bank[:, 0:width])
+                    else:
+                        nc.vector.tensor_tensor(out=top[:, 0:width], in0=bank[:, 0:width], in1=top[:, 0:width], op=MAX)
+            for (w, grp, col, width), top in zip(units, best):
+                bias_q = bias[:, grp * 512 + col : grp * 512 + col + width]
+                engine = nc.vector if add_engine == "V" else nc.gpsimd
+                engine.tensor_tensor(out=top[:, 0:width], in0=top[:, 0:width], in1=bias_q, op=ADD)
+                h0 = 8 * grp + col // 64
+                heads = width // 64
                 nc.sync.dma_start(
-                    out=out_0[0, h0 + a : h0 + a + 4, w, :, :].rearrange("h i d -> i h d"),
-                    in_=best_h[:, a : a + 4, :],
+                    out=out_0[0, h0 : h0 + heads, w, :, :].rearrange("h i d -> i h d"),
+                    in_=top[:, 0:width].rearrange("p (h d) -> p h d", d=64),
                 )
 
         bias_rows = const.tile([P, 512], BF16, name="bias_rows")
         ident_bf = const.tile([P, P], BF16, name="ident_bf")
         ident = const.tile([P, P], F32, name="ident")
-        bias = const.tile([P, 3072], F32, name="bias")
-
+        bias = const.tile([P, 3072], BF16, name="bias")
         zeros = const.tile([P, 512], BF16, name="zeros")
-        nc.vector.memset(bias_rows[:], 0.0)
-        nc.vector.memset(zeros[:], 0.0)
+        nc.vector.memset(bias_rows[:].bitcast(U32), 0)
+        nc.vector.memset(zeros[:].bitcast(U32), 0)
         load(("w", 2), 4, 0, 2)
         nc.sync.dma_start(out=bias_rows[0:6, :], in_=qkv_b.rearrange("(n c) -> n c", n=6))
         load(("w", 2), 4, 2, 4)
         load(("x", 0), 4)
         load(("x", 1), 2)
         load(("x", 2), 2)
-        load(("w", 3), 1)
-        load(("w", 4), 1)
+        for idx in (3, 4, 5, 0, 1):
+            load(("w", idx), 1)
         make_identity(nc, ident_bf[:])
         make_identity(nc, ident[:])
+        for w in range(3):
+            new_codes(("x", w))
+            new_codes(("q", w))
+        for idx in range(6):
+            new_codes(("w", idx))
+
+        def transpose_pair(w, pair):
+            for t in (2 * pair, 2 * pair + 1):
+                transpose_tile(("x", w), t, "S")
 
         warm = psum.tile([P, 512], F32, name="bank")
-        for i in range(4):
+        for i in range(3):
             nc.tensor.matmul(warm[:], lhsT=ident_bf[:], rhs=zeros[:], start=True, stop=True)
-        prepare_fine(("w", 2), "SVSV", {1: ((2, "V"), (3, "S")), 3: ((4, "S"), (5, "V"))})
-        load(("w", 5), 1)
-        prepare_fine(("x", 0), "SSVS", {1: ((0, "S"), (1, "S"))})
-        load(("w", 0), 1)
-        kv_unit(2, 0, "VVVV", tiles=(0, 1))
-        prepare(("x", 1), "SVSV")
-        load(("w", 1), 1)
-        kv_unit(2, 0, "VVVV", tiles=(2, 3))
-        quantise_whole(("x", 1))
-        prepare(("x", 2), "SVSV")
-        kv_unit(2, 1, "VVVS", ("x", 2))
-        prepare(("w", 3), "SSSS")
-        kv_unit(2, 2, "VVVS", ("w", 3))
-        prepare(("w", 4), "SSSS")
-        kv_unit(3, 0, "VVVS", ("w", 4))
-        prepare(("w", 5), "SSSS")
-        kv_unit(3, 1, "VVVS", ("w", 5))
-        prepare(("w", 0), "SSSS")
-        kv_unit(3, 2, "VVVS", ("w", 0))
-        prepare(("w", 1), "SSSS")
-        kv_unit(4, 0, "VVVS", ("w", 1))
-        kv_unit(4, 1, "VVVS", ("q", 0), 2)
-        kv_unit(4, 2, "VVVS", ("q", 1), 2)
-        kv_unit(5, 0, "VVVS", ("q", 2), 2)
-        q_unit(0, 0, "G")
+        transpose_tile(("w", 2), 0, "S")
+        transpose_tile(("w", 2), 1, "V")
+        quantise_w_half(2, 0)
+        transpose_tile(("w", 2), 2, "S")
+        transpose_tile(("w", 2), 3, "V")
+        transpose_tile(("x", 0), 0, "S")
+        quantise_w_half(2, 1)
+        quantise_x_tile(0, 0)
+        spread_bias(2, "V")
+        transpose_tile(("x", 0), 1, "S")
+        quantise_x_tile(0, 1)
+        transpose_pair(0, 1)
+        kv_matmul(2, 0, 0)
+        quantise_x_pair(0, 1)
+        kv_finish(2, 0, 0, "V")
+        transpose_pair(1, 0)
+        kv_matmul(2, 0, 1)
+        quantise_x_pair(1, 0)
+        kv_finish(2, 0, 1, "V")
+
+        steps = [(w, pair) for w in range(3) for pair in range(2)]
+        for i in range(1, 6):
+            w, pair = steps[i]
+            ahead = steps[i + 2] if i < 4 else None
+            if ahead:
+                transpose_pair(*ahead)
+            elif i == 4:
+                for t in range(4):
+                    transpose_tile(("w", 3), t, "SVSV"[t])
+            for j in (2 * pair, 2 * pair + 1):
+                kv_matmul(2, w, j)
+            if ahead:
+                quantise_x_pair(*ahead)
+            elif i == 4:
+                quantise_w(3)
+            if i in (1, 2, 3):
+                spread_bias(2 + i, "S")
+            kv_finish(2, w, 2 * pair, "V")
+            kv_finish(2, w, 2 * pair + 1, "V" if i < 4 else "S")
+
+        def prepare(idx):
+            for t in range(4):
+                transpose_tile(("w", idx), t, "S")
+
+        prepare(4)
+        kv_unit(3, 0, "VVVS", lambda: quantise_w(4))
+        kv_unit(3, 1, "VSVS", lambda: move_for_q(0))
+        prepare(5)
+        kv_unit(3, 2, "VVVS", lambda: quantise_w(5))
+        spread_bias(0, "S")
+        kv_unit(4, 0, "VSVS", lambda: move_for_q(1))
+        prepare(0)
+        kv_unit(4, 1, "VVVS", lambda: quantise_w(0))
+        spread_bias(1, "S")
+        kv_unit(4, 2, "VSVS", lambda: move_for_q(2))
+        prepare(1)
+        kv_unit(5, 0, "VVVS", lambda: quantise_w(1))
         kv_unit(5, 1, "VSVS")
-        q_unit(1, 0, "G")
         kv_unit(5, 2, "VSVS")
-        q_unit(2, 0, "G")
-        q_unit(0, 1, "G")
-        q_unit(1, 1, "G")
-        q_unit(2, 1, "G", 0, 256)
-        q_unit(2, 1, "V", 256, 256)
+
+        q_units(((0, 0, 0, 512), (1, 0, 0, 512)), "G")
+        q_units(((2, 0, 0, 512), (0, 1, 0, 512)), "G")
+        q_units(((1, 1, 0, 512), (2, 1, 0, 256)), "G")
+        q_units(((2, 1, 256, 128), (2, 1, 384, 128)), "V")

@@ -217,52 +217,54 @@ def tile_hieramaskunitattention_pa_kernel(tc, embeddings, qkv_w, qkv_b, out_0, o
         for idx in range(6):
             new_codes(("w", idx))
 
-        def transpose_pair(w, pair):
-            for t in (2 * pair, 2 * pair + 1):
-                transpose_tile(("x", w), t, "S")
+        def transpose_x(w, engines):
+            for t in range(4):
+                transpose_tile(("x", w), t, engines[t])
 
         warm = psum.tile([P, 512], F32, name="bank")
-        for i in range(3):
+        for i in range(4):
             nc.tensor.matmul(warm[:], lhsT=ident_bf[:], rhs=zeros[:], start=True, stop=True)
         transpose_tile(("w", 2), 0, "S")
         transpose_tile(("w", 2), 1, "V")
+        spread_bias(2, "S")
         quantise_w_half(2, 0)
-        transpose_tile(("w", 2), 2, "S")
-        transpose_tile(("w", 2), 3, "V")
-        transpose_tile(("x", 0), 0, "S")
+        transpose_tile(("w", 2), 2, "V")
+        spread_bias(3, "S")
+        transpose_tile(("w", 2), 3, "S")
+        spread_bias(4, "V")
         quantise_w_half(2, 1)
+        transpose_tile(("x", 0), 0, "S")
+        spread_bias(5, "S")
         quantise_x_tile(0, 0)
-        spread_bias(2, "V")
         transpose_tile(("x", 0), 1, "S")
         quantise_x_tile(0, 1)
-        transpose_pair(0, 1)
+        transpose_tile(("x", 0), 2, "V")
+        transpose_tile(("x", 0), 3, "S")
+        spread_bias(0, "S")
         kv_matmul(2, 0, 0)
-        quantise_x_pair(0, 1)
-        kv_finish(2, 0, 0, "V")
-        transpose_pair(1, 0)
         kv_matmul(2, 0, 1)
-        quantise_x_pair(1, 0)
+        quantise_x_pair(0, 1)
+        spread_bias(1, "S")
+        kv_finish(2, 0, 0, "V")
         kv_finish(2, 0, 1, "V")
-
-        steps = [(w, pair) for w in range(3) for pair in range(2)]
-        for i in range(1, 6):
-            w, pair = steps[i]
-            ahead = steps[i + 2] if i < 4 else None
-            if ahead:
-                transpose_pair(*ahead)
-            elif i == 4:
-                for t in range(4):
-                    transpose_tile(("w", 3), t, "SVSV"[t])
-            for j in (2 * pair, 2 * pair + 1):
-                kv_matmul(2, w, j)
-            if ahead:
-                quantise_x_pair(*ahead)
-            elif i == 4:
-                quantise_w(3)
-            if i in (1, 2, 3):
-                spread_bias(2 + i, "S")
-            kv_finish(2, w, 2 * pair, "V")
-            kv_finish(2, w, 2 * pair + 1, "V" if i < 4 else "S")
+        transpose_x(1, "SSSS")
+        kv_matmul(2, 0, 2)
+        kv_matmul(2, 0, 3)
+        quantise_x_pair(1, 0)
+        kv_finish(2, 0, 2, "V")
+        quantise_x_pair(1, 1)
+        kv_finish(2, 0, 3, "V")
+        transpose_x(2, "SVSV")
+        for j in range(4):
+            kv_matmul(2, 1, j)
+        quantise_x_pair(2, 0)
+        kv_finish(2, 1, 0, "V")
+        quantise_x_pair(2, 1)
+        for j, engine in zip((1, 2, 3), "VVS"):
+            kv_finish(2, 1, j, engine)
+        for t in range(4):
+            transpose_tile(("w", 3), t, "SSSS"[t])
+        kv_unit(2, 2, "VVVS", lambda: quantise_w(3))
 
         def prepare(idx):
             for t in range(4):
@@ -273,11 +275,9 @@ def tile_hieramaskunitattention_pa_kernel(tc, embeddings, qkv_w, qkv_b, out_0, o
         kv_unit(3, 1, "VSVS", lambda: move_for_q(0))
         prepare(5)
         kv_unit(3, 2, "VVVS", lambda: quantise_w(5))
-        spread_bias(0, "S")
         kv_unit(4, 0, "VSVS", lambda: move_for_q(1))
         prepare(0)
         kv_unit(4, 1, "VVVS", lambda: quantise_w(0))
-        spread_bias(1, "S")
         kv_unit(4, 2, "VSVS", lambda: move_for_q(2))
         prepare(1)
         kv_unit(5, 0, "VVVS", lambda: quantise_w(1))

from contextlib import ExitStack

import concourse.mybir as mybir
from concourse.masks import make_identity

F32 = mybir.dt.float32
BF16 = mybir.dt.bfloat16
U32 = mybir.dt.uint32
I32 = mybir.dt.int32
U8 = mybir.dt.uint8
FP8X4 = mybir.dt.float8_e4m3fn_x4
ADD = mybir.AluOpType.add
MAX = mybir.AluOpType.max

P = 128
FLOPS = 2 * 1536 * 3072 * 1024


def tile_hieramaskunitattention_pa_kernel(tc, embeddings, qkv_w, qkv_b, out_0, out_1, out_2):
    nc = tc.nc
    x_rows = embeddings.flatten_outer_dims().rearrange("(p j w) k -> w p j k", j=4, w=3)

    with ExitStack() as ctx:
        const = ctx.enter_context(tc.tile_pool(name="const", bufs=1))
        raw_pool = ctx.enter_context(tc.tile_pool(name="raw", bufs=9))
        grp_w_pool = ctx.enter_context(tc.tile_pool(name="grpw", bufs=2))
        grp_x_pool = ctx.enter_context(tc.tile_pool(name="grpx", bufs=3))
        code_pool = ctx.enter_context(tc.tile_pool(name="code", bufs=1))
        out_pool = ctx.enter_context(tc.tile_pool(name="outp", bufs=6))
        qo_pool = ctx.enter_context(tc.tile_pool(name="qo", bufs=6))
        psum = ctx.enter_context(tc.psum_pool(name="psum", bufs=8))
        ctx.enter_context(tc.manual_schedule())

        raws = {}
        grouped = {}
        codes = {}
        planes = {}
        banks = {}
        results = {}

        def load(key, pieces, first=0, last=4):
            kind, idx = key
            if key not in raws:
                raws[key] = raw_pool.tile([P, 4096], BF16, name="raw", align_bytes=64)
            view = raws[key][:].rearrange("p (t k) -> p t k", t=4)
            if kind == "x":
                src = x_rows[idx]
            else:
                src = qkv_w[512 * idx : 512 * idx + 512, :].rearrange("(t p) k -> p t k", p=P)
            step = 4 // pieces
            for a in range(first, last, step):
                nc.sync.dma_start(out=view[:, a : a + step, :], in_=src[:, a : a + step, :])

        def new_codes(key):
            codes[key] = code_pool.tile([P, 1024], U32, name="codes_%s%d" % key, align_bytes=64)
            planes[key] = code_pool.tile([P, 1024], U8, name="plane_%s%d" % key, align_bytes=64)
            if key[0] == "x":
                nc.gpsimd.memset(planes[key][:].bitcast(U32), 0)

        def copy_out(engine, out, in_):
            if engine == "S":
                nc.scalar.copy(out=out, in_=in_)
            else:
                nc.vector.tensor_copy(out=out, in_=in_)

        def transpose_tile(key, t, engine):
            if key[0] == "x":
                if t % 2 == 0:
                    grouped[key + (t // 2,)] = grp_x_pool.tile([P, 2048], BF16, name="grouped_x", align_bytes=64)
                dst = grouped[key + (t // 2,)][:].bitcast(F32)
                dst = dst.rearrange("p (t g n u) -> p t g n u", t=2, g=2, n=P, u=2)[:, t % 2, :, :, :]
            else:
                if t == 0:
                    grouped[key] = grp_w_pool.tile([P, 4096], BF16, name="grouped_w", align_bytes=64)
                dst = grouped[key][:].bitcast(F32)
                dst = dst.rearrange("p (g t n u) -> p g t n u", g=2, t=4, n=P, u=2)[:, :, t, :, :]
            words = raws[key][:].bitcast(F32)
            bank = psum.tile([P, 512], F32, name="bank")
            for gu in range(4):
                nc.tensor.transpose(
                    bank[:, gu * P : (gu + 1) * P],
                    words[:, t * 512 + gu * P : t * 512 + (gu + 1) * P],
                    ident[:],
                )
            copy_out(engine, dst, bank[:].rearrange("p (g u n) -> p g n u", g=2, u=2, n=P))

        def quantise(key, first, width, source):
            nc.vector.quantize_mx(
                out=codes[key][:, first : first + width].bitcast(FP8X4),
                scales=planes[key][:, first : first + width],
                in_=source,
            )

        def quantise_w(idx):
            key = ("w", idx)
            quantise(key, 0, 1024, grouped[key][:])

        def quantise_w_half(idx, half):
            key = ("w", idx)
            for g in range(2):
                a = 512 * g + 256 * half
                quantise(key, a, 256, grouped[key][:, 4 * a : 4 * a + 1024])

        def quantise_x_pair(w, pair):
            key = ("x", w)
            quantise(key, 512 * pair, 512, grouped[key + (pair,)][:])

        def quantise_x_tile(w, t):
            key = ("x", w)
            a = 1024 * (t % 2)
            quantise(key, 256 * t, 256, grouped[key + (t // 2,)][:, a : a + 1024])

        def move_for_q(w):
            for table, dtype in ((codes, I32), (planes, U8)):
                nc.vector.tensor_copy(
                    out=table[("q", w)][:].bitcast(dtype).rearrange("p (c t) -> p c t", t=4),
                    in_=table[("x", w)][:].bitcast(dtype).rearrange("p (t c) -> p c t", t=4),
                )

        def spread_bias(n, engine):
            bank = psum.tile([P, 512], F32, name="bank")
            nc.tensor.matmul(
                bank[:], lhsT=ident_bf[:, n : n + 1].to_broadcast([P, P]), rhs=bias_rows[:], start=True, stop=True
            )
            copy_out(engine, bias[:, n * 512 : (n + 1) * 512], bank[:])

        def mx_pair(bank, stat_key, stat, mov_key, mov_col=0, width=512):
            for g in range(2):
                s0 = (2 * stat + g) * P if stat_key[0] == "x" else (4 * g + stat) * P
                m0 = g * 512 + mov_col
                nc.tensor.matmul_mx(
                    out=bank[:, 0:width],
                    lhsT=codes[stat_key][:, s0 : s0 + P].bitcast(FP8X4),
                    lhsT_scale=planes[stat_key][:, s0 : s0 + P],
                    rhs=codes[mov_key][:, m0 : m0 + width].bitcast(FP8X4),
                    rhs_scale=planes[mov_key][:, m0 : m0 + width],
                    start=(g == 0),
                    stop=(g == 1),
                )

        def kv_matmul(grp, w, j):
            bank = psum.tile([P, 512], F32, name="bank")
            mx_pair(bank, ("x", w), j, ("w", grp))
            banks[(grp, w, j)] = bank

        def kv_finish(grp, w, j, engine):
            if j == 0:
                results[(grp, w)] = out_pool.tile([P, 2048], F32, name="res")
            res = results[(grp, w)]
            part = res[:].rearrange("p (h j d) -> p h j d", h=8, j=4, d=64)[:, :, j, :]
            bank_v = banks[(grp, w, j)][:].rearrange("p (h d) -> p h d", h=8)
            bias_v = bias[:, grp * 512 : (grp + 1) * 512].rearrange("p (h d) -> p h d", h=8)
            if engine == "V":
                nc.vector.tensor_tensor(out=part, in0=bank_v, in1=bias_v, op=ADD)
            else:
                nc.scalar.copy(out=part, in_=bank_v)
                nc.gpsimd.tensor_tensor(out=part, in0=part, in1=bias_v, op=ADD)
            if j == 3:
                dram = out_1 if grp < 4 else out_2
                h0 = 8 * (grp % 2)
                res_h = res[:].rearrange("p (h e) -> p h e", h=8)
                for a in (0, 4):
                    nc.sync.dma_start(
                        out=dram[0, h0 + a : h0 + a + 4, w, :, :].rearrange("h (p j) d -> p h (j d)", j=4),
                        in_=res_h[:, a : a + 4, :],
                    )

        def kv_unit(grp, w, engines, between=None):
            for j in range(4):
                kv_matmul(grp, w, j)
            for j in range(4):
                kv_finish(grp, w, j, engines[j])
                if between is not None and j == 0:
                    between()

        def q_units(units, add_engine):
            best = [qo_pool.tile([P, 512], F32, name="best") for unit in units]
            for g in range(4):
                for (w, grp, col, width), top in zip(units, best):
                    bank = psum.tile([P, 512], F32, name="bank")
                    mx_pair(bank, ("q", w), g, ("w", grp), col, width)
                    if g == 0:
                        nc.scalar.copy(out=top[:, 0:width], in_=bank[:, 0:width])
                    else:
                        nc.vector.tensor_tensor(out=top[:, 0:width], in0=bank[:, 0:width], in1=top[:, 0:width], op=MAX)
            for (w, grp, col, width), top in zip(units, best):
                bias_q = bias[:, grp * 512 + col : grp * 512 + col + width]
                engine = nc.vector if add_engine == "V" else nc.gpsimd
                engine.tensor_tensor(out=top[:, 0:width], in0=top[:, 0:width], in1=bias_q, op=ADD)
                h0 = 8 * grp + col // 64
                heads = width // 64
                nc.sync.dma_start(
                    out=out_0[0, h0 : h0 + heads, w, :, :].rearrange("h i d -> i h d"),
                    in_=top[:, 0:width].rearrange("p (h d) -> p h d", d=64),
                )

        bias_rows = const.tile([P, 512], BF16, name="bias_rows")
        ident_bf = const.tile([P, P], BF16, name="ident_bf")
        ident = const.tile([P, P], F32, name="ident")
        bias = const.tile([P, 3072], BF16, name="bias")
        zeros = const.tile([P, 512], BF16, name="zeros")
        nc.vector.memset(bias_rows[:].bitcast(U32), 0)
        nc.vector.memset(zeros[:].bitcast(U32), 0)
        load(("w", 2), 4, 0, 2)
        nc.sync.dma_start(out=bias_rows[0:6, :], in_=qkv_b.rearrange("(n c) -> n c", n=6))
        load(("w", 2), 4, 2, 4)
        load(("x", 0), 4)
        load(("x", 1), 2)
        load(("x", 2), 2)
        for idx in (3, 4, 5, 0, 1):
            load(("w", idx), 1)
        make_identity(nc, ident_bf[:])
        make_identity(nc, ident[:])
        for w in range(3):
            new_codes(("x", w))
            new_codes(("q", w))
        for idx in range(6):
            new_codes(("w", idx))

        def transpose_x(w, engines):
            for t in range(4):
                transpose_tile(("x", w), t, engines[t])

        warm = psum.tile([P, 512], F32, name="bank")
        for i in range(4):
            nc.tensor.matmul(warm[:], lhsT=ident_bf[:], rhs=zeros[:], start=True, stop=True)
        transpose_tile(("w", 2), 0, "S")
        transpose_tile(("w", 2), 1, "V")
        spread_bias(2, "S")
        quantise_w_half(2, 0)
        transpose_tile(("w", 2), 2, "V")
        spread_bias(3, "S")
        transpose_tile(("w", 2), 3, "S")
        spread_bias(4, "V")
        quantise_w_half(2, 1)
        transpose_tile(("x", 0), 0, "S")
        spread_bias(5, "S")
        quantise_x_tile(0, 0)
        transpose_tile(("x", 0), 1, "S")
        quantise_x_tile(0, 1)
        transpose_tile(("x", 0), 2, "V")
        transpose_tile(("x", 0), 3, "S")
        spread_bias(0, "S")
        kv_matmul(2, 0, 0)
        kv_matmul(2, 0, 1)
        quantise_x_pair(0, 1)
        spread_bias(1, "S")
        kv_finish(2, 0, 0, "V")
        kv_finish(2, 0, 1, "V")
        transpose_x(1, "SSSS")
        kv_matmul(2, 0, 2)
        kv_matmul(2, 0, 3)
        quantise_x_pair(1, 0)
        kv_finish(2, 0, 2, "V")
        quantise_x_pair(1, 1)
        kv_finish(2, 0, 3, "V")
        transpose_x(2, "SVSV")
        for j in range(4):
            kv_matmul(2, 1, j)
        quantise_x_pair(2, 0)
        kv_finish(2, 1, 0, "V")
        quantise_x_pair(2, 1)
        for j, engine in zip((1, 2, 3), "VVS"):
            kv_finish(2, 1, j, engine)
        for t in range(4):
            transpose_tile(("w", 3), t, "SSSS"[t])
        kv_unit(2, 2, "VVVS", lambda: quantise_w(3))

        def prepare(idx):
            for t in range(4):
                transpose_tile(("w", idx), t, "S")

        prepare(4)
        kv_unit(3, 0, "VVVS", lambda: quantise_w(4))
        kv_unit(3, 1, "VSVS", lambda: move_for_q(0))
        prepare(5)
        kv_unit(3, 2, "VVVS", lambda: quantise_w(5))
        kv_unit(4, 0, "VSVS", lambda: move_for_q(1))
        prepare(0)
        kv_unit(4, 1, "VVVS", lambda: quantise_w(0))
        kv_unit(4, 2, "VSVS", lambda: move_for_q(2))
        prepare(1)
        kv_unit(5, 0, "VVVS", lambda: quantise_w(1))
        kv_unit(5, 1, "VSVS")
        kv_unit(5, 2, "VSVS")

        q_units(((0, 0, 0, 512), (1, 0, 0, 512)), "G")
        q_units(((2, 0, 0, 512), (0, 1, 0, 512)), "G")
        q_units(((1, 1, 0, 512), (2, 1, 0, 256)), "G")
        q_units(((2, 1, 256, 128), (2, 1, 384, 128)), "V")
